import numpy as np
import ml_dtypes


def mxq(x, axis, fmt="e4m3"):
    dtype, down = {"e4m3": (ml_dtypes.float8_e4m3fn, 7), "e5m2": (ml_dtypes.float8_e5m2, 14)}[fmt]
    v = np.moveaxis(np.asarray(x, np.float32).astype(ml_dtypes.bfloat16).astype(np.float64), axis, -1)
    blocks = v.reshape(v.shape[:-1] + (-1, 32))
    amax = np.abs(blocks).max(-1, keepdims=True)
    byte = np.maximum(np.where(amax > 0, np.frexp(amax)[1] - 1 + 127, 0) - down, 1)
    scale = np.exp2(byte - 127.0)
    codes = (blocks / scale).astype(np.float32).astype(dtype).astype(np.float64)
    return np.moveaxis((codes * scale).reshape(v.shape), -1, axis)


WIDE = False


def mx_kscale(k):
    if not WIDE:
        return np.ones(k)
    levels = np.array([10, -10, 5, -5, 0])
    a = np.random.permutation(np.resize(levels, k // 512 * 4)).reshape(k // 512, 4)
    idx = np.arange(k)
    return np.exp2(a[idx // 512, idx % 128 // 32])


BF16 = ml_dtypes.bfloat16


def bf(x):
    return np.asarray(x, np.float32).astype(BF16)


def f64(x):
    return np.asarray(x).astype(np.float64)


E2M1 = np.array([0.0, 0.5, 1.0, 1.5, 2.0, 3.0, 4.0, 6.0, -0.0, -0.5, -1.0, -1.5, -2.0, -3.0, -4.0, -6.0])


def pack_weight(w, fmt):
    k, n = w.shape
    w = f64(bf(w)).reshape(k // 32, 32, n)
    amax = np.abs(w).max(1)
    if fmt == "e4m3":
        byte = np.frexp(amax)[1] - 1 + 127 - 7
    else:
        mant, ex = np.frexp(amax / 6.0)
        byte = np.where(mant > 0.5, ex, ex - 1) + 127
    byte = np.clip(np.where(amax > 0, byte, 1), 1, 254)
    scaled = (w * np.exp2(127.0 - byte)[:, None, :]).reshape(k, n).astype(np.float32)
    by_word = np.ascontiguousarray(scaled.reshape(k // 512, 128, 4, n).transpose(0, 1, 3, 2))
    if fmt == "e4m3":
        words = by_word.astype(ml_dtypes.float8_e4m3fn).view(np.uint8)
    else:
        c = by_word.astype(ml_dtypes.float4_e2m1fn).view(np.uint8) & 0xF
        words = c[..., 0::2] | (c[..., 1::2] << 4)
    return np.ascontiguousarray(words), np.ascontiguousarray(byte.astype(np.uint8).reshape(k // 512, 16, n))


def unpack_weight(words, scales, fmt):
    g, p, n, _ = words.shape
    if fmt == "e4m3":
        vals = np.ascontiguousarray(words).view(ml_dtypes.float8_e4m3fn).astype(np.float64)
    else:
        nib = np.empty((g, p, n, 4), np.uint8)
        nib[..., 0::2] = words & 0xF
        nib[..., 1::2] = words >> 4
        vals = E2M1[nib]
    vals = vals * np.repeat(np.exp2(scales.astype(np.float64) - 127.0), 8, axis=1)[..., None]
    return vals.transpose(0, 1, 3, 2).reshape(g * 512, n)

def pack4(w):
    words, scales = pack_weight(w, "e2m1")
    return words.reshape(words.shape[0], 128, -1), scales


def unpack4(words, scales):
    return unpack_weight(words.reshape(words.shape[0], 128, -1, 2), scales, "e2m1")


B, NH, T, D, N, CK = 1, 2, 8192, 256, 256, 512
KD = NH * N
EPS_LN = 1e-5
TARGET_ACTIVITY = 0.1


def layernorm(v):
    m = np.mean(v, axis=-1, keepdims=True)
    var = np.mean((v - m) ** 2, axis=-1, keepdims=True)
    return (v - m) / np.sqrt(var + EPS_LN)


def setup_inputs():
    t = mx_kscale(KD)
    xy = np.maximum(np.random.standard_normal((B, NH, T, N)) * 0.5, 0.0) * np.maximum(np.random.standard_normal((B, NH, T, N)), 0.0)
    xy_sparse = bf(xy * t.reshape(NH, 1, N))
    decoder_words, decoder_scales = pack4(np.random.standard_normal((KD, D)) * 2.0 / np.sqrt(KD) / t[:, None])
    return {'xy_sparse': xy_sparse,
            'decoder_words': decoder_words,
            'decoder_scales': decoder_scales,
            'x': bf(np.random.standard_normal((B, 1, T, D))),
            'scale': bf(1.0 + 0.1 * np.random.standard_normal(D)),
            'running_activity': bf(TARGET_ACTIVITY * np.exp(0.5 * np.random.standard_normal(D)))}


def reference(xy_sparse, decoder_words, decoder_scales, x, scale, running_activity):
    flat = f64(xy_sparse).transpose(0, 2, 1, 3).reshape(B, 1, T, KD)
    y_mlp = mxq(flat, 3, 'e4m3') @ unpack4(decoder_words, decoder_scales)
    y = layernorm(y_mlp)
    regulation = TARGET_ACTIVITY / (f64(running_activity) + 1e-6)
    y = y * np.sqrt(regulation) * f64(scale)
    return layernorm(f64(x) + y)

@@ -1,0 +1,276 @@
+import concourse.mybir as mybir
+from concourse.masks import make_identity
+
+F32 = mybir.dt.float32
+BF16 = mybir.dt.bfloat16
+I32 = mybir.dt.int32
+U32 = mybir.dt.uint32
+U8 = mybir.dt.uint8
+FP8X4 = mybir.dt.float8_e4m3fn_x4
+FP4X4 = mybir.dt.float4_e2m1fn_x4
+ALU = mybir.AluOpType
+ACT = mybir.ActivationFunctionType
+
+P = 128
+HEADS = 2
+HEAD_DIM = 256
+K = HEADS * HEAD_DIM
+PACK = 4
+D = 256
+T = 8192
+TILES = T // P
+GROUP = 4
+GROUPS = TILES // GROUP
+BANK_TILES = 2
+BANKS = GROUP // BANK_TILES
+PSUM_BANKS = 8
+BN_STATS_DIM = 6
+BN_AGGR_DIM = 2
+EPS_LN = 1e-5
+TARGET_ACTIVITY = 0.1
+
+FLOPS = 2 * T * K * D
+
+
+def tile_bdhlayer_pc_t_kernel(
+    tc, xy_sparse, decoder_words, decoder_scales, x, scale, running_activity, out
+):
+    nc = tc.nc
+
+    xy_view = xy_sparse[0].rearrange("h (p j) n -> h p j n", p=P)
+    x_view = x[0, 0].rearrange("(p j) d -> p j d", p=P)
+    out_view = out[0, 0].rearrange("(p j) d -> p j d", p=P)
+
+    with tc.tile_pool(name="const", bufs=1) as const, tc.tile_pool(
+        name="inputs", bufs=GROUPS
+    ) as inputs, tc.tile_pool(name="quant", bufs=3) as quant, tc.tile_pool(
+        name="rows", bufs=6
+    ) as rows, tc.tile_pool(name="small", bufs=6) as small, tc.psum_pool(
+        name="turned_banks", bufs=PSUM_BANKS // 2
+    ) as turned_banks, tc.psum_pool(
+        name="decoded_banks", bufs=PSUM_BANKS // 2
+    ) as decoded_banks, tc.manual_schedule():
+        flat_of = {}
+        x_of = {}
+        turned_of = {}
+        grouped_of = {}
+        codes_of = {}
+        decoded_of = {}
+        row_of = {}
+        stat_of = {}
+
+        def load(g):
+            tiles = slice(g * GROUP, (g + 1) * GROUP)
+            flat = inputs.tile([P, GROUP, HEADS, HEAD_DIM], BF16, name="flat")
+            for h in range(HEADS):
+                nc.sync.dma_start(out=flat[:, :, h, :], in_=xy_view[h, :, tiles, :])
+            flat_of[g] = flat
+            x_sb = inputs.tile([P, GROUP, D], BF16, name="x_sb")
+            nc.sync.dma_start(out=x_sb[:], in_=x_view[:, tiles, :])
+            x_of[g] = x_sb
+
+        ident = const.tile([P, P], F32, name="ident")
+        make_identity(nc, ident[:])
+
+        w_scales = const.tile([P, D], U8, name="w_scales", align_bytes=64)
+        nc.vector.memset(w_scales[:].bitcast(I32), 0)
+        w_words = const.tile([P, 2 * D], U8, name="w_words", align_bytes=64)
+
+        activity = const.tile([P, D], BF16, name="activity")
+        nc.scalar.dma_start(out=activity[:], in_=running_activity.partition_broadcast(P))
+        trained = const.tile([P, D], BF16, name="trained")
+        nc.scalar.dma_start(out=trained[:], in_=scale.partition_broadcast(P))
+
+        load(0)
+        nc.sync.dma_start(out=w_words[:].bitcast(I32), in_=decoder_words[0].bitcast(I32))
+        for quadrant in range(4):
+            nc.sync.dma_start(
+                out=w_scales[32 * quadrant : 32 * quadrant + 4, :].bitcast(I32),
+                in_=decoder_scales[0, 4 * quadrant : 4 * quadrant + 4, :].bitcast(I32),
+            )
+        for g in range(1, GROUPS):
+            load(g)
+
+        gain = const.tile([P, D], F32, name="gain")
+        nc.scalar.activation(
+            out=gain[:],
+            in_=activity[:],
+            func=ACT.Abs_reciprocal_sqrt,
+            scale=1.0 / TARGET_ACTIVITY,
+            bias=1e-6 / TARGET_ACTIVITY,
+        )
+        nc.vector.tensor_mul(out=gain[:], in0=gain[:], in1=trained[:])
+
+        def turn(g):
+            words = flat_of[g][:].rearrange("p j h n -> p (j h n)").bitcast(F32)
+            row_words = K // 2
+            turned_of[g] = []
+            for b in range(BANKS):
+                turned = turned_banks.tile([P, BANK_TILES, 2, P], F32, name="turned")
+                for i in range(BANK_TILES):
+                    first = (b * BANK_TILES + i) * row_words
+                    for u in range(2):
+                        nc.tensor.transpose(
+                            turned[:, i, u, :],
+                            words[:, first + u : first + row_words : 2],
+                            ident[:],
+                        )
+                turned_of[g].append(turned)
+
+        def regroup(g):
+            grouped = quant.tile([P, GROUP, P, PACK], BF16, name="grouped", align_bytes=64)
+            grouped_words = (
+                grouped[:]
+                .rearrange("p j r t -> p (j r t)")
+                .bitcast(F32)
+                .rearrange("p (j r u) -> p j r u", j=GROUP, u=2)
+            )
+            for b in range(BANKS):
+                nc.scalar.copy(
+                    out=grouped_words[:, b * BANK_TILES : (b + 1) * BANK_TILES, :, :],
+                    in_=turned_of[g][b][:].rearrange("p i u r -> p i r u"),
+                )
+            grouped_of[g] = grouped
+
+        def quantise(g):
+            codes = quant.tile([P, GROUP * P], U32, name="codes", align_bytes=64)
+            code_scales = quant.tile([P, GROUP * P], U8, name="code_scales", align_bytes=64)
+            nc.vector.quantize_mx(
+                out=codes[:].bitcast(FP8X4),
+                scales=code_scales[:],
+                in_=grouped_of[g][:].rearrange("p j r t -> p (j r t)"),
+            )
+            codes_of[g] = (codes, code_scales)
+
+        def decode(g):
+            codes, code_scales = codes_of[g]
+            decoded_of[g] = []
+            for b in range(BANKS):
+                decoded = decoded_banks.tile([P, BANK_TILES, D], F32, name="decoded")
+                for i in range(BANK_TILES):
+                    j = b * BANK_TILES + i
+                    tokens = slice(j * P, (j + 1) * P)
+                    nc.tensor.matmul_mx(
+                        out=decoded[:, i, :],
+                        lhsT=codes[:, tokens].bitcast(FP8X4),
+                        lhsT_scale=code_scales[:, tokens],
+                        rhs=w_words[:].bitcast(FP4X4),
+                        rhs_scale=w_scales[:],
+                        start=True,
+                        stop=True,
+                    )
+                decoded_of[g].append(decoded)
+
+        def first_stats(g):
+            stats = small.tile([P, GROUP, BN_STATS_DIM], F32, name="stats")
+            mean_var = small.tile([P, GROUP, BN_AGGR_DIM], F32, name="mean_var")
+            for j in range(GROUP):
+                y_mlp = decoded_of[g][j // BANK_TILES][:, j % BANK_TILES, :]
+                nc.vector.bn_stats(out=stats[:, j, :], in_=y_mlp)
+            for j in range(GROUP):
+                nc.vector.bn_aggr(out=mean_var[:, j, :], in_=stats[:, j, :])
+            stat_of[g] = {"mean_var": mean_var}
+
+        def first_rstd(g):
+            rstd1 = small.tile([P, GROUP], F32, name="rstd1")
+            nc.scalar.activation(
+                out=rstd1[:],
+                in_=stat_of[g]["mean_var"][:, :, 1],
+                func=ACT.Abs_reciprocal_sqrt,
+                bias=EPS_LN,
+            )
+            stat_of[g]["rstd1"] = rstd1
+
+        def first_apply(g):
+            row = rows.tile([P, GROUP, D], F32, name="row")
+            for j in range(GROUP):
+                nc.vector.scalar_tensor_tensor(
+                    out=row[:, j, :],
+                    in0=decoded_of[g][j // BANK_TILES][:, j % BANK_TILES, :],
+                    scalar=stat_of[g]["mean_var"][:, j, 0:1],
+                    in1=gain[:],
+                    op0=ALU.subtract,
+                    op1=ALU.mult,
+                )
+            row_of[g] = row
+
+        def residual(g):
+            row = row_of[g]
+            row_sum = small.tile([P, GROUP], F32, name="row_sum")
+            for j in range(GROUP):
+                nc.vector.scalar_tensor_tensor(
+                    out=row[:, j, :],
+                    in0=row[:, j, :],
+                    scalar=stat_of[g]["rstd1"][:, j : j + 1],
+                    in1=x_of[g][:, j, :],
+                    op0=ALU.mult,
+                    op1=ALU.add,
+                    accum_out=row_sum[:, j : j + 1],
+                )
+            neg_mean = small.tile([P, GROUP], F32, name="neg_mean")
+            nc.vector.tensor_scalar_mul(out=neg_mean[:], in0=row_sum[:], scalar1=-1.0 / D)
+            stat_of[g]["neg_mean"] = neg_mean
+
+        def second_stats(g):
+            squares = quant.tile([P, GROUP, D], BF16, name="squares")
+            dev_sum = small.tile([P, GROUP], F32, name="dev_sum")
+            for j in range(GROUP):
+                nc.scalar.activation(
+                    out=squares[:, j, :],
+                    in_=row_of[g][:, j, :],
+                    func=ACT.Square,
+                    bias=stat_of[g]["neg_mean"][:, j : j + 1],
+                    accum_out=dev_sum[:, j : j + 1],
+                )
+            rstd2 = small.tile([P, GROUP], F32, name="rstd2")
+            nc.scalar.activation(
+                out=rstd2[:],
+                in_=dev_sum[:],
+                func=ACT.Abs_reciprocal_sqrt,
+                scale=1.0 / D,
+                bias=EPS_LN,
+            )
+            stat_of[g]["rstd2"] = rstd2
+
+        def second_shift(g):
+            shift = small.tile([P, GROUP], F32, name="shift")
+            nc.vector.tensor_mul(
+                out=shift[:], in0=stat_of[g]["neg_mean"][:], in1=stat_of[g]["rstd2"][:]
+            )
+            stat_of[g]["shift"] = shift
+
+        def finish(g):
+            row = row_of[g]
+            for j in range(GROUP):
+                nc.scalar.activation(
+                    out=row[:, j, :],
+                    in_=row[:, j, :],
+                    func=ACT.Identity,
+                    scale=stat_of[g]["rstd2"][:, j : j + 1],
+                    bias=stat_of[g]["shift"][:, j : j + 1],
+                )
+            nc.sync.dma_start(out=out_view[:, g * GROUP : (g + 1) * GROUP, :], in_=row[:])
+
+        def valid(g):
+            return 0 <= g < GROUPS
+
+        for g in range(-3, GROUPS + 3):
+            if valid(g + 2):
+                regroup(g + 2)
+            if valid(g + 3):
+                turn(g + 3)
+            if valid(g + 1):
+                quantise(g + 1)
+                decode(g + 1)
+            if valid(g - 2):
+                second_stats(g - 2)
+            if valid(g):
+                first_stats(g)
+                first_rstd(g)
+                first_apply(g)
+            if valid(g - 1):
+                residual(g - 1)
+            if valid(g - 2):
+                second_shift(g - 2)
+            if valid(g - 3):
+                finish(g - 3)

@@ -242,12 +242,13 @@ def tile_bdhlayer_pc_t_kernel(
         def finish(g):
             row = row_of[g]
             for j in range(GROUP):
-                nc.scalar.activation(
+                nc.gpsimd.tensor_scalar(
                     out=row[:, j, :],
-                    in_=row[:, j, :],
-                    func=ACT.Identity,
-                    scale=stat_of[g]["rstd2"][:, j : j + 1],
-                    bias=stat_of[g]["shift"][:, j : j + 1],
+                    in0=row[:, j, :],
+                    scalar1=stat_of[g]["rstd2"][:, j : j + 1],
+                    scalar2=stat_of[g]["shift"][:, j : j + 1],
+                    op0=ALU.mult,
+                    op1=ALU.add,
                 )
             nc.sync.dma_start(out=out_view[:, g * GROUP : (g + 1) * GROUP, :], in_=row[:])
 

@@ -161,37 +161,79 @@ def tile_bdhlayer_pc_t_kernel(
                     )
                 decoded_of[g].append(decoded)
 
-        def first_stats(g):
-            stats = small.tile([P, GROUP, BN_STATS_DIM], F32, name="stats")
-            mean_var = small.tile([P, GROUP, BN_AGGR_DIM], F32, name="mean_var")
-            for j in range(GROUP):
-                y_mlp = decoded_of[g][j // BANK_TILES][:, j % BANK_TILES, :]
-                nc.vector.bn_stats(out=stats[:, j, :], in_=y_mlp)
-            for j in range(GROUP):
-                nc.vector.bn_aggr(out=mean_var[:, j, :], in_=stats[:, j, :])
-            stat_of[g] = {"mean_var": mean_var}
+        def first_stats_vector(g):
+            stats = small.tile([P, BANK_TILES, BN_STATS_DIM], F32, name="stats")
+            for i in range(BANK_TILES):
+                nc.vector.bn_stats(out=stats[:, i, :], in_=decoded_of[g][0][:, i, :])
+            stat_of[g] = {"stats": stats}
+
+        def first_aggr_vector(g):
+            mean_var = small.tile([P, BANK_TILES, BN_AGGR_DIM], F32, name="mean_var")
+            for i in range(BANK_TILES):
+                nc.vector.bn_aggr(out=mean_var[:, i, :], in_=stat_of[g]["stats"][:, i, :])
+            stat_of[g]["mean_var"] = mean_var
+
+        def first_sums_scalar(g):
+            scrap = quant.tile([P, 2, BANK_TILES, D], BF16, name="scrap")
+            sum1 = small.tile([P, BANK_TILES], F32, name="sum1")
+            for i in range(BANK_TILES):
+                nc.scalar.activation(
+                    out=scrap[:, 0, i, :],
+                    in_=decoded_of[g][1][:, i, :],
+                    func=ACT.Identity,
+                    accum_out=sum1[:, i : i + 1],
+                )
+            stat_of[g]["scrap"] = scrap
+            stat_of[g]["sum1"] = sum1
+
+        def first_mean_scalar(g):
+            mean1 = small.tile([P, BANK_TILES], F32, name="mean1")
+            nc.scalar.mul(out=mean1[:], in_=stat_of[g]["sum1"][:], mul=1.0 / D)
+            stat_of[g]["mean1"] = mean1
+
+        def first_devs_scalar(g):
+            dev1 = small.tile([P, BANK_TILES], F32, name="dev1")
+            for i in range(BANK_TILES):
+                nc.scalar.activation(
+                    out=stat_of[g]["scrap"][:, 1, i, :],
+                    in_=decoded_of[g][1][:, i, :],
+                    func=ACT.Square,
+                    scale=-1.0,
+                    bias=stat_of[g]["mean1"][:, i : i + 1],
+                    accum_out=dev1[:, i : i + 1],
+                )
+            stat_of[g]["dev1"] = dev1
 
         def first_rstd(g):
             rstd1 = small.tile([P, GROUP], F32, name="rstd1")
             nc.scalar.activation(
-                out=rstd1[:],
+                out=rstd1[:, 0:BANK_TILES],
                 in_=stat_of[g]["mean_var"][:, :, 1],
                 func=ACT.Abs_reciprocal_sqrt,
+                bias=EPS_LN,
+            )
+            nc.scalar.activation(
+                out=rstd1[:, BANK_TILES:GROUP],
+                in_=stat_of[g]["dev1"][:],
+                func=ACT.Abs_reciprocal_sqrt,
+                scale=1.0 / D,
                 bias=EPS_LN,
             )
             stat_of[g]["rstd1"] = rstd1
 
         def first_apply(g):
             row = rows.tile([P, GROUP, D], F32, name="row")
-            for j in range(GROUP):
-                nc.vector.scalar_tensor_tensor(
-                    out=row[:, j, :],
-                    in0=decoded_of[g][j // BANK_TILES][:, j % BANK_TILES, :],
-                    scalar=stat_of[g]["mean_var"][:, j, 0:1],
-                    in1=gain[:],
-                    op0=ALU.subtract,
-                    op1=ALU.mult,
-                )
+            means = [stat_of[g]["mean_var"][:, :, 0], stat_of[g]["mean1"][:]]
+            for b in reversed(range(BANKS)):
+                for i in range(BANK_TILES):
+                    nc.vector.scalar_tensor_tensor(
+                        out=row[:, b * BANK_TILES + i, :],
+                        in0=decoded_of[g][b][:, i, :],
+                        scalar=means[b][:, i : i + 1],
+                        in1=gain[:],
+                        op0=ALU.subtract,
+                        op1=ALU.mult,
+                    )
             row_of[g] = row
 
         def residual(g):
@@ -207,46 +249,52 @@ def tile_bdhlayer_pc_t_kernel(
                     op1=ALU.add,
                     accum_out=row_sum[:, j : j + 1],
                 )
+            stat_of[g]["row_sum"] = row_sum
+
+        def second_mean(g):
             neg_mean = small.tile([P, GROUP], F32, name="neg_mean")
-            nc.vector.tensor_scalar_mul(out=neg_mean[:], in0=row_sum[:], scalar1=-1.0 / D)
+            nc.scalar.mul(out=neg_mean[:], in_=stat_of[g]["row_sum"][:], mul=-1.0 / D)
             stat_of[g]["neg_mean"] = neg_mean
 
-        def second_stats(g):
+        def second_devs(g):
             squares = quant.tile([P, GROUP, D], BF16, name="squares")
-            dev_sum = small.tile([P, GROUP], F32, name="dev_sum")
+            dev2 = small.tile([P, GROUP], F32, name="dev2")
             for j in range(GROUP):
                 nc.scalar.activation(
                     out=squares[:, j, :],
                     in_=row_of[g][:, j, :],
                     func=ACT.Square,
                     bias=stat_of[g]["neg_mean"][:, j : j + 1],
-                    accum_out=dev_sum[:, j : j + 1],
+                    accum_out=dev2[:, j : j + 1],
                 )
+            stat_of[g]["dev2"] = dev2
+
+        def second_rstd(g):
             rstd2 = small.tile([P, GROUP], F32, name="rstd2")
             nc.scalar.activation(
                 out=rstd2[:],
-                in_=dev_sum[:],
+                in_=stat_of[g]["dev2"][:],
                 func=ACT.Abs_reciprocal_sqrt,
                 scale=1.0 / D,
                 bias=EPS_LN,
             )
             stat_of[g]["rstd2"] = rstd2
 
-        def second_shift(g):
-            shift = small.tile([P, GROUP], F32, name="shift")
-            nc.vector.tensor_mul(
-                out=shift[:], in0=stat_of[g]["neg_mean"][:], in1=stat_of[g]["rstd2"][:]
-            )
-            stat_of[g]["shift"] = shift
-
         def finish(g):
             row = row_of[g]
+            shift = small.tile([P, GROUP], F32, name="shift")
+            nc.gpsimd.tensor_tensor(
+                out=shift[:],
+                in0=stat_of[g]["neg_mean"][:],
+                in1=stat_of[g]["rstd2"][:],
+                op=ALU.mult,
+            )
             for j in range(GROUP):
                 nc.gpsimd.tensor_scalar(
                     out=row[:, j, :],
                     in0=row[:, j, :],
                     scalar1=stat_of[g]["rstd2"][:, j : j + 1],
-                    scalar2=stat_of[g]["shift"][:, j : j + 1],
+                    scalar2=shift[:, j : j + 1],
                     op0=ALU.mult,
                     op1=ALU.add,
                 )
@@ -256,22 +304,32 @@ def tile_bdhlayer_pc_t_kernel(
             return 0 <= g < GROUPS
 
         for g in range(-3, GROUPS + 3):
+            if valid(g + 1):
+                quantise(g + 1)
+                decode(g + 1)
+            if valid(g):
+                first_stats_vector(g)
+                first_sums_scalar(g)
             if valid(g + 2):
                 regroup(g + 2)
             if valid(g + 3):
                 turn(g + 3)
-            if valid(g + 1):
-                quantise(g + 1)
-                decode(g + 1)
-            if valid(g - 2):
-                second_stats(g - 2)
             if valid(g):
-                first_stats(g)
-                first_rstd(g)
-                first_apply(g)
+                first_mean_scalar(g)
+            if valid(g - 2):
+                second_mean(g - 2)
+            if valid(g):
+                first_devs_scalar(g)
+            if valid(g - 2):
+                second_devs(g - 2)
             if valid(g - 1):
                 residual(g - 1)
+            if valid(g):
+                first_aggr_vector(g)
+                first_rstd(g)
             if valid(g - 2):
-                second_shift(g - 2)
+                second_rstd(g - 2)
+            if valid(g):
+                first_apply(g)
             if valid(g - 3):
                 finish(g - 3)

@@ -186,9 +186,9 @@ def tile_bdhlayer_pc_t_kernel(
             stat_of[g]["scrap"] = scrap
             stat_of[g]["sum1"] = sum1
 
-        def first_mean_scalar(g):
+        def first_mean(g):
             mean1 = small.tile([P, BANK_TILES], F32, name="mean1")
-            nc.scalar.mul(out=mean1[:], in_=stat_of[g]["sum1"][:], mul=1.0 / D)
+            nc.vector.tensor_scalar_mul(out=mean1[:], in0=stat_of[g]["sum1"][:], scalar1=1.0 / D)
             stat_of[g]["mean1"] = mean1
 
         def first_devs_scalar(g):
@@ -253,7 +253,7 @@ def tile_bdhlayer_pc_t_kernel(
 
         def second_mean(g):
             neg_mean = small.tile([P, GROUP], F32, name="neg_mean")
-            nc.scalar.mul(out=neg_mean[:], in_=stat_of[g]["row_sum"][:], mul=-1.0 / D)
+            nc.vector.tensor_scalar_mul(out=neg_mean[:], in0=stat_of[g]["row_sum"][:], scalar1=-1.0 / D)
             stat_of[g]["neg_mean"] = neg_mean
 
         def second_devs(g):
@@ -314,10 +314,10 @@ def tile_bdhlayer_pc_t_kernel(
                 regroup(g + 2)
             if valid(g + 3):
                 turn(g + 3)
-            if valid(g):
-                first_mean_scalar(g)
             if valid(g - 2):
                 second_mean(g - 2)
+            if valid(g):
+                first_mean(g)
             if valid(g):
                 first_devs_scalar(g)
             if valid(g - 2):

@@ -25,7 +25,8 @@ BANK_TILES = 2
 BANKS = GROUP // BANK_TILES
 PSUM_BANKS = 8
 BN_STATS_DIM = 6
-BN_AGGR_DIM = 2
+MEAN = 1
+DEVIATIONS = 2
 EPS_LN = 1e-5
 TARGET_ACTIVITY = 0.1
 
@@ -161,60 +162,20 @@ def tile_bdhlayer_pc_t_kernel(
                     )
                 decoded_of[g].append(decoded)
 
-        def first_stats_vector(g):
-            stats = small.tile([P, BANK_TILES, BN_STATS_DIM], F32, name="stats")
-            for i in range(BANK_TILES):
-                nc.vector.bn_stats(out=stats[:, i, :], in_=decoded_of[g][0][:, i, :])
+        def first_stats(g):
+            stats = small.tile([P, BANKS, BANK_TILES, BN_STATS_DIM // 2], F32, name="stats")
+            for b in range(BANKS):
+                nc.vector.bn_stats(
+                    out=stats[:, b, :, :].rearrange("p i s -> p (i s)"),
+                    in_=decoded_of[g][b][:].rearrange("p i d -> p d i"),
+                )
             stat_of[g] = {"stats": stats}
-
-        def first_aggr_vector(g):
-            mean_var = small.tile([P, BANK_TILES, BN_AGGR_DIM], F32, name="mean_var")
-            for i in range(BANK_TILES):
-                nc.vector.bn_aggr(out=mean_var[:, i, :], in_=stat_of[g]["stats"][:, i, :])
-            stat_of[g]["mean_var"] = mean_var
-
-        def first_sums_scalar(g):
-            scrap = quant.tile([P, 2, BANK_TILES, D], BF16, name="scrap")
-            sum1 = small.tile([P, BANK_TILES], F32, name="sum1")
-            for i in range(BANK_TILES):
-                nc.scalar.activation(
-                    out=scrap[:, 0, i, :],
-                    in_=decoded_of[g][1][:, i, :],
-                    func=ACT.Identity,
-                    accum_out=sum1[:, i : i + 1],
-                )
-            stat_of[g]["scrap"] = scrap
-            stat_of[g]["sum1"] = sum1
-
-        def first_mean(g):
-            mean1 = small.tile([P, BANK_TILES], F32, name="mean1")
-            nc.vector.tensor_scalar_mul(out=mean1[:], in0=stat_of[g]["sum1"][:], scalar1=1.0 / D)
-            stat_of[g]["mean1"] = mean1
-
-        def first_devs_scalar(g):
-            dev1 = small.tile([P, BANK_TILES], F32, name="dev1")
-            for i in range(BANK_TILES):
-                nc.scalar.activation(
-                    out=stat_of[g]["scrap"][:, 1, i, :],
-                    in_=decoded_of[g][1][:, i, :],
-                    func=ACT.Square,
-                    scale=-1.0,
-                    bias=stat_of[g]["mean1"][:, i : i + 1],
-                    accum_out=dev1[:, i : i + 1],
-                )
-            stat_of[g]["dev1"] = dev1
 
         def first_rstd(g):
             rstd1 = small.tile([P, GROUP], F32, name="rstd1")
             nc.scalar.activation(
-                out=rstd1[:, 0:BANK_TILES],
-                in_=stat_of[g]["mean_var"][:, :, 1],
-                func=ACT.Abs_reciprocal_sqrt,
-                bias=EPS_LN,
-            )
-            nc.scalar.activation(
-                out=rstd1[:, BANK_TILES:GROUP],
-                in_=stat_of[g]["dev1"][:],
+                out=rstd1[:].rearrange("p (b i) -> p b i", i=BANK_TILES),
+                in_=stat_of[g]["stats"][:, :, :, DEVIATIONS],
                 func=ACT.Abs_reciprocal_sqrt,
                 scale=1.0 / D,
                 bias=EPS_LN,
@@ -223,13 +184,12 @@ def tile_bdhlayer_pc_t_kernel(
 
         def first_apply(g):
             row = rows.tile([P, GROUP, D], F32, name="row")
-            means = [stat_of[g]["mean_var"][:, :, 0], stat_of[g]["mean1"][:]]
-            for b in reversed(range(BANKS)):
+            for b in range(BANKS):
                 for i in range(BANK_TILES):
                     nc.vector.scalar_tensor_tensor(
                         out=row[:, b * BANK_TILES + i, :],
                         in0=decoded_of[g][b][:, i, :],
-                        scalar=means[b][:, i : i + 1],
+                        scalar=stat_of[g]["stats"][:, b, i, MEAN : MEAN + 1],
                         in1=gain[:],
                         op0=ALU.subtract,
                         op1=ALU.mult,
@@ -308,27 +268,20 @@ def tile_bdhlayer_pc_t_kernel(
                 quantise(g + 1)
                 decode(g + 1)
             if valid(g):
-                first_stats_vector(g)
-                first_sums_scalar(g)
+                first_stats(g)
             if valid(g + 2):
                 regroup(g + 2)
             if valid(g + 3):
                 turn(g + 3)
             if valid(g - 2):
                 second_mean(g - 2)
-            if valid(g):
-                first_mean(g)
-            if valid(g):
-                first_devs_scalar(g)
-            if valid(g - 2):
                 second_devs(g - 2)
-            if valid(g - 1):
-                residual(g - 1)
             if valid(g):
-                first_aggr_vector(g)
                 first_rstd(g)
             if valid(g - 2):
                 second_rstd(g - 2)
+            if valid(g - 1):
+                residual(g - 1)
             if valid(g):
                 first_apply(g)
             if valid(g - 3):

@@ -19,6 +19,8 @@ PACK = 4
 D = 256
 T = 8192
 TILES = T // P
+LOAD_TILES = 4
+LOADS = TILES // LOAD_TILES
 GROUP = 4
 GROUPS = TILES // GROUP
 BANK_TILES = 2
@@ -43,7 +45,7 @@ def tile_bdhlayer_pc_t_kernel(
     out_view = out[0, 0].rearrange("(p j) d -> p j d", p=P)
 
     with tc.tile_pool(name="const", bufs=1) as const, tc.tile_pool(
-        name="inputs", bufs=GROUPS
+        name="inputs", bufs=LOADS
     ) as inputs, tc.tile_pool(name="quant", bufs=3) as quant, tc.tile_pool(
         name="rows", bufs=6
     ) as rows, tc.tile_pool(name="small", bufs=6) as small, tc.psum_pool(
@@ -60,15 +62,15 @@ def tile_bdhlayer_pc_t_kernel(
         row_of = {}
         stat_of = {}
 
-        def load(g):
-            tiles = slice(g * GROUP, (g + 1) * GROUP)
-            flat = inputs.tile([P, GROUP, HEADS, HEAD_DIM], BF16, name="flat")
+        def load(n):
+            tiles = slice(n * LOAD_TILES, (n + 1) * LOAD_TILES)
+            flat = inputs.tile([P, LOAD_TILES, HEADS, HEAD_DIM], BF16, name="flat")
             for h in range(HEADS):
                 nc.sync.dma_start(out=flat[:, :, h, :], in_=xy_view[h, :, tiles, :])
-            flat_of[g] = flat
-            x_sb = inputs.tile([P, GROUP, D], BF16, name="x_sb")
+            flat_of[n] = flat
+            x_sb = inputs.tile([P, LOAD_TILES, D], BF16, name="x_sb")
             nc.sync.dma_start(out=x_sb[:], in_=x_view[:, tiles, :])
-            x_of[g] = x_sb
+            x_of[n] = x_sb
 
         ident = const.tile([P, P], F32, name="ident")
         make_identity(nc, ident[:])
@@ -76,11 +78,8 @@ def tile_bdhlayer_pc_t_kernel(
         w_scales = const.tile([P, D], U8, name="w_scales", align_bytes=64)
         nc.vector.memset(w_scales[:].bitcast(I32), 0)
         w_words = const.tile([P, 2 * D], U8, name="w_words", align_bytes=64)
-
         activity = const.tile([P, D], BF16, name="activity")
-        nc.scalar.dma_start(out=activity[:], in_=running_activity.partition_broadcast(P))
         trained = const.tile([P, D], BF16, name="trained")
-        nc.scalar.dma_start(out=trained[:], in_=scale.partition_broadcast(P))
 
         load(0)
         nc.sync.dma_start(out=w_words[:].bitcast(I32), in_=decoder_words[0].bitcast(I32))
@@ -89,27 +88,32 @@ def tile_bdhlayer_pc_t_kernel(
                 out=w_scales[32 * quadrant : 32 * quadrant + 4, :].bitcast(I32),
                 in_=decoder_scales[0, 4 * quadrant : 4 * quadrant + 4, :].bitcast(I32),
             )
-        for g in range(1, GROUPS):
-            load(g)
+        nc.sync.dma_start(out=activity[:], in_=running_activity.partition_broadcast(P))
+        nc.sync.dma_start(out=trained[:], in_=scale.partition_broadcast(P))
+        for n in range(1, LOADS):
+            load(n)
 
         gain = const.tile([P, D], F32, name="gain")
-        nc.scalar.activation(
-            out=gain[:],
-            in_=activity[:],
-            func=ACT.Abs_reciprocal_sqrt,
-            scale=1.0 / TARGET_ACTIVITY,
-            bias=1e-6 / TARGET_ACTIVITY,
-        )
-        nc.vector.tensor_mul(out=gain[:], in0=gain[:], in1=trained[:])
+
+        def make_gain():
+            nc.scalar.activation(
+                out=gain[:],
+                in_=activity[:],
+                func=ACT.Abs_reciprocal_sqrt,
+                scale=1.0 / TARGET_ACTIVITY,
+                bias=1e-6 / TARGET_ACTIVITY,
+            )
+            nc.gpsimd.tensor_tensor(out=gain[:], in0=gain[:], in1=trained[:], op=ALU.mult)
 
         def turn(g):
-            words = flat_of[g][:].rearrange("p j h n -> p (j h n)").bitcast(F32)
+            first_tile = g * GROUP
+            words = flat_of[first_tile // LOAD_TILES][:].rearrange("p j h n -> p (j h n)").bitcast(F32)
             row_words = K // 2
             turned_of[g] = []
             for b in range(BANKS):
                 turned = turned_banks.tile([P, BANK_TILES, 2, P], F32, name="turned")
                 for i in range(BANK_TILES):
-                    first = (b * BANK_TILES + i) * row_words
+                    first = (first_tile % LOAD_TILES + b * BANK_TILES + i) * row_words
                     for u in range(2):
                         nc.tensor.transpose(
                             turned[:, i, u, :],
@@ -198,13 +202,15 @@ def tile_bdhlayer_pc_t_kernel(
 
         def residual(g):
             row = row_of[g]
+            first_tile = g * GROUP
+            x_sb = x_of[first_tile // LOAD_TILES]
             row_sum = small.tile([P, GROUP], F32, name="row_sum")
             for j in range(GROUP):
                 nc.vector.scalar_tensor_tensor(
                     out=row[:, j, :],
                     in0=row[:, j, :],
                     scalar=stat_of[g]["rstd1"][:, j : j + 1],
-                    in1=x_of[g][:, j, :],
+                    in1=x_sb[:, first_tile % LOAD_TILES + j, :],
                     op0=ALU.mult,
                     op1=ALU.add,
                     accum_out=row_sum[:, j : j + 1],
@@ -242,28 +248,39 @@ def tile_bdhlayer_pc_t_kernel(
 
         def finish(g):
             row = row_of[g]
+            rstd2 = stat_of[g]["rstd2"]
             shift = small.tile([P, GROUP], F32, name="shift")
             nc.gpsimd.tensor_tensor(
-                out=shift[:],
-                in0=stat_of[g]["neg_mean"][:],
-                in1=stat_of[g]["rstd2"][:],
-                op=ALU.mult,
+                out=shift[:], in0=stat_of[g]["neg_mean"][:], in1=rstd2[:], op=ALU.mult
             )
-            for j in range(GROUP):
+            for j in range(0, GROUP, 2):
                 nc.gpsimd.tensor_scalar(
                     out=row[:, j, :],
                     in0=row[:, j, :],
-                    scalar1=stat_of[g]["rstd2"][:, j : j + 1],
+                    scalar1=rstd2[:, j : j + 1],
                     scalar2=shift[:, j : j + 1],
                     op0=ALU.mult,
                     op1=ALU.add,
                 )
-            nc.sync.dma_start(out=out_view[:, g * GROUP : (g + 1) * GROUP, :], in_=row[:])
+                nc.scalar.activation(
+                    out=row[:, j + 1, :],
+                    in_=row[:, j + 1, :],
+                    func=ACT.Identity,
+                    scale=rstd2[:, j + 1 : j + 2],
+                    bias=shift[:, j + 1 : j + 2],
+                )
+                nc.sync.dma_start(
+                    out=out_view[:, g * GROUP + j : g * GROUP + j + 2, :], in_=row[:, j : j + 2, :]
+                )
 
         def valid(g):
             return 0 <= g < GROUPS
 
-        for g in range(-3, GROUPS + 3):
+        turn(0)
+        regroup(0)
+        turn(1)
+        make_gain()
+        for g in range(-1, GROUPS + 3):
             if valid(g + 1):
                 quantise(g + 1)
                 decode(g + 1)

@@ -166,20 +166,51 @@ def tile_bdhlayer_pc_t_kernel(
                     )
                 decoded_of[g].append(decoded)
 
-        def first_stats(g):
-            stats = small.tile([P, BANKS, BANK_TILES, BN_STATS_DIM // 2], F32, name="stats")
-            for b in range(BANKS):
-                nc.vector.bn_stats(
-                    out=stats[:, b, :, :].rearrange("p i s -> p (i s)"),
-                    in_=decoded_of[g][b][:].rearrange("p i d -> p d i"),
-                )
+        def first_stats_vector(g):
+            stats = small.tile([P, GROUP, BN_STATS_DIM // 2], F32, name="stats")
+            nc.vector.bn_stats(
+                out=stats[:, 0:BANK_TILES, :].rearrange("p i s -> p (i s)"),
+                in_=decoded_of[g][0][:].rearrange("p i d -> p d i"),
+            )
             stat_of[g] = {"stats": stats}
+
+        def first_sums_scalar(g):
+            y_sum = small.tile([P, BANK_TILES], F32, name="y_sum")
+            for i in range(BANK_TILES):
+                unused = quant.tile([P, D], BF16, name="unused")
+                nc.scalar.activation(
+                    out=unused[:],
+                    in_=decoded_of[g][1][:, i, :],
+                    func=ACT.Identity,
+                    accum_out=y_sum[:, i : i + 1],
+                )
+            stat_of[g]["y_sum"] = y_sum
+
+        def first_mean_scalar(g):
+            nc.scalar.activation(
+                out=stat_of[g]["stats"][:, BANK_TILES:GROUP, MEAN],
+                in_=stat_of[g]["y_sum"][:],
+                func=ACT.Copy,
+                scale=1.0 / D,
+            )
+
+        def first_devs_scalar(g):
+            for i in range(BANK_TILES):
+                unused = quant.tile([P, D], BF16, name="unused")
+                nc.scalar.activation(
+                    out=unused[:],
+                    in_=decoded_of[g][1][:, i, :],
+                    func=ACT.Square,
+                    scale=-1.0,
+                    bias=stat_of[g]["stats"][:, BANK_TILES + i, MEAN : MEAN + 1],
+                    accum_out=stat_of[g]["stats"][:, BANK_TILES + i, DEVIATIONS : DEVIATIONS + 1],
+                )
 
         def first_rstd(g):
             rstd1 = small.tile([P, GROUP], F32, name="rstd1")
             nc.scalar.activation(
-                out=rstd1[:].rearrange("p (b i) -> p b i", i=BANK_TILES),
-                in_=stat_of[g]["stats"][:, :, :, DEVIATIONS],
+                out=rstd1[:],
+                in_=stat_of[g]["stats"][:, :, DEVIATIONS],
                 func=ACT.Abs_reciprocal_sqrt,
                 scale=1.0 / D,
                 bias=EPS_LN,
@@ -188,12 +219,13 @@ def tile_bdhlayer_pc_t_kernel(
 
         def first_apply(g):
             row = rows.tile([P, GROUP, D], F32, name="row")
-            for b in range(BANKS):
+            for b in reversed(range(BANKS)):
                 for i in range(BANK_TILES):
+                    j = b * BANK_TILES + i
                     nc.vector.scalar_tensor_tensor(
-                        out=row[:, b * BANK_TILES + i, :],
+                        out=row[:, j, :],
                         in0=decoded_of[g][b][:, i, :],
-                        scalar=stat_of[g]["stats"][:, b, i, MEAN : MEAN + 1],
+                        scalar=stat_of[g]["stats"][:, j, MEAN : MEAN + 1],
                         in1=gain[:],
                         op0=ALU.subtract,
                         op1=ALU.mult,
@@ -254,21 +286,15 @@ def tile_bdhlayer_pc_t_kernel(
                 out=shift[:], in0=stat_of[g]["neg_mean"][:], in1=rstd2[:], op=ALU.mult
             )
             for j in range(0, GROUP, 2):
-                nc.gpsimd.tensor_scalar(
-                    out=row[:, j, :],
-                    in0=row[:, j, :],
-                    scalar1=rstd2[:, j : j + 1],
-                    scalar2=shift[:, j : j + 1],
-                    op0=ALU.mult,
-                    op1=ALU.add,
-                )
-                nc.scalar.activation(
-                    out=row[:, j + 1, :],
-                    in_=row[:, j + 1, :],
-                    func=ACT.Identity,
-                    scale=rstd2[:, j + 1 : j + 2],
-                    bias=shift[:, j + 1 : j + 2],
-                )
+                for i in range(2):
+                    nc.gpsimd.tensor_scalar(
+                        out=row[:, j + i, :],
+                        in0=row[:, j + i, :],
+                        scalar1=rstd2[:, j + i : j + i + 1],
+                        scalar2=shift[:, j + i : j + i + 1],
+                        op0=ALU.mult,
+                        op1=ALU.add,
+                    )
                 nc.sync.dma_start(
                     out=out_view[:, g * GROUP + j : g * GROUP + j + 2, :], in_=row[:, j : j + 2, :]
                 )
@@ -285,11 +311,15 @@ def tile_bdhlayer_pc_t_kernel(
                 quantise(g + 1)
                 decode(g + 1)
             if valid(g):
-                first_stats(g)
+                first_stats_vector(g)
+                first_sums_scalar(g)
             if valid(g + 2):
                 regroup(g + 2)
             if valid(g + 3):
                 turn(g + 3)
+            if valid(g):
+                first_mean_scalar(g)
+                first_devs_scalar(g)
             if valid(g - 2):
                 second_mean(g - 2)
                 second_devs(g - 2)

@@ -165,14 +165,16 @@ def tile_bdhlayer_pc_t_kernel(
                         stop=True,
                     )
                 decoded_of[g].append(decoded)
+            stats = small.tile([P, GROUP, BN_STATS_DIM // 2], F32, name="stats")
+            stat_of[g] = {"stats": stats}
 
         def first_stats_vector(g):
-            stats = small.tile([P, GROUP, BN_STATS_DIM // 2], F32, name="stats")
-            nc.vector.bn_stats(
-                out=stats[:, 0:BANK_TILES, :].rearrange("p i s -> p (i s)"),
-                in_=decoded_of[g][0][:].rearrange("p i d -> p d i"),
-            )
-            stat_of[g] = {"stats": stats}
+            stats = stat_of[g]["stats"]
+            for b in range(BANKS - 1 if scalar_takes(g) else BANKS):
+                nc.vector.bn_stats(
+                    out=stats[:, b * BANK_TILES : (b + 1) * BANK_TILES, :].rearrange("p i s -> p (i s)"),
+                    in_=decoded_of[g][b][:].rearrange("p i d -> p d i"),
+                )
 
         def first_sums_scalar(g):
             y_sum = small.tile([P, BANK_TILES], F32, name="y_sum")
@@ -219,7 +221,7 @@ def tile_bdhlayer_pc_t_kernel(
 
         def first_apply(g):
             row = rows.tile([P, GROUP, D], F32, name="row")
-            for b in reversed(range(BANKS)):
+            for b in range(BANKS):
                 for i in range(BANK_TILES):
                     j = b * BANK_TILES + i
                     nc.vector.scalar_tensor_tensor(
@@ -232,12 +234,14 @@ def tile_bdhlayer_pc_t_kernel(
                     )
             row_of[g] = row
 
-        def residual(g):
+        def residual(g, first=0, last=GROUP):
             row = row_of[g]
             first_tile = g * GROUP
             x_sb = x_of[first_tile // LOAD_TILES]
-            row_sum = small.tile([P, GROUP], F32, name="row_sum")
-            for j in range(GROUP):
+            if first == 0:
+                row_sum = small.tile([P, GROUP], F32, name="row_sum")
+                stat_of[g]["row_sum"] = row_sum
+            for j in range(first, last):
                 nc.vector.scalar_tensor_tensor(
                     out=row[:, j, :],
                     in0=row[:, j, :],
@@ -245,38 +249,50 @@ def tile_bdhlayer_pc_t_kernel(
                     in1=x_sb[:, first_tile % LOAD_TILES + j, :],
                     op0=ALU.mult,
                     op1=ALU.add,
-                    accum_out=row_sum[:, j : j + 1],
+                    accum_out=stat_of[g]["row_sum"][:, j : j + 1],
                 )
-            stat_of[g]["row_sum"] = row_sum
 
-        def second_mean(g):
-            neg_mean = small.tile([P, GROUP], F32, name="neg_mean")
-            nc.vector.tensor_scalar_mul(out=neg_mean[:], in0=stat_of[g]["row_sum"][:], scalar1=-1.0 / D)
-            stat_of[g]["neg_mean"] = neg_mean
+        def second_mean(g, first=0, last=GROUP):
+            if first == 0:
+                neg_mean = small.tile([P, GROUP], F32, name="neg_mean")
+                stat_of[g]["neg_mean"] = neg_mean
+            nc.vector.tensor_scalar_mul(
+                out=stat_of[g]["neg_mean"][:, first:last],
+                in0=stat_of[g]["row_sum"][:, first:last],
+                scalar1=-1.0 / D,
+            )
 
-        def second_devs(g):
-            squares = quant.tile([P, GROUP, D], BF16, name="squares")
-            dev2 = small.tile([P, GROUP], F32, name="dev2")
-            for j in range(GROUP):
+        def second_devs(g, first=0, last=GROUP):
+            if first == 0:
+                squares = quant.tile([P, GROUP, D], BF16, name="squares")
+                dev2 = small.tile([P, GROUP], F32, name="dev2")
+                stat_of[g]["squares"] = squares
+                stat_of[g]["dev2"] = dev2
+            for j in range(first, last):
                 nc.scalar.activation(
-                    out=squares[:, j, :],
+                    out=stat_of[g]["squares"][:, j, :],
                     in_=row_of[g][:, j, :],
                     func=ACT.Square,
                     bias=stat_of[g]["neg_mean"][:, j : j + 1],
-                    accum_out=dev2[:, j : j + 1],
+                    accum_out=stat_of[g]["dev2"][:, j : j + 1],
                 )
-            stat_of[g]["dev2"] = dev2
 
-        def second_rstd(g):
-            rstd2 = small.tile([P, GROUP], F32, name="rstd2")
+        def second_rstd(g, first=0, last=GROUP):
+            if first == 0:
+                rstd2 = small.tile([P, GROUP], F32, name="rstd2")
+                stat_of[g]["rstd2"] = rstd2
             nc.scalar.activation(
-                out=rstd2[:],
-                in_=stat_of[g]["dev2"][:],
+                out=stat_of[g]["rstd2"][:, first:last],
+                in_=stat_of[g]["dev2"][:, first:last],
                 func=ACT.Abs_reciprocal_sqrt,
                 scale=1.0 / D,
                 bias=EPS_LN,
             )
-            stat_of[g]["rstd2"] = rstd2
+
+        def store(g, j):
+            nc.sync.dma_start(
+                out=out_view[:, g * GROUP + j : g * GROUP + j + 2, :], in_=row_of[g][:, j : j + 2, :]
+            )
 
         def finish(g):
             row = row_of[g]
@@ -285,51 +301,84 @@ def tile_bdhlayer_pc_t_kernel(
             nc.gpsimd.tensor_tensor(
                 out=shift[:], in0=stat_of[g]["neg_mean"][:], in1=rstd2[:], op=ALU.mult
             )
-            for j in range(0, GROUP, 2):
-                for i in range(2):
-                    nc.gpsimd.tensor_scalar(
-                        out=row[:, j + i, :],
-                        in0=row[:, j + i, :],
-                        scalar1=rstd2[:, j + i : j + i + 1],
-                        scalar2=shift[:, j + i : j + i + 1],
-                        op0=ALU.mult,
-                        op1=ALU.add,
-                    )
-                nc.sync.dma_start(
-                    out=out_view[:, g * GROUP + j : g * GROUP + j + 2, :], in_=row[:, j : j + 2, :]
+            for j in range(GROUP):
+                nc.gpsimd.tensor_scalar(
+                    out=row[:, j, :],
+                    in0=row[:, j, :],
+                    scalar1=rstd2[:, j : j + 1],
+                    scalar2=shift[:, j : j + 1],
+                    op0=ALU.mult,
+                    op1=ALU.add,
                 )
+                if j % 2 == 1:
+                    store(g, j - 1)
+
+        def finish_on_vector(g, first=0, last=GROUP):
+            row = row_of[g]
+            for j in range(first, last):
+                nc.vector.tensor_scalar(
+                    out=row[:, j, :],
+                    in0=row[:, j, :],
+                    scalar1=stat_of[g]["neg_mean"][:, j : j + 1],
+                    scalar2=stat_of[g]["rstd2"][:, j : j + 1],
+                    op0=ALU.add,
+                    op1=ALU.mult,
+                )
+                if j % 2 == 1:
+                    store(g, j - 1)
 
         def valid(g):
             return 0 <= g < GROUPS
+
+        def scalar_takes(g):
+            return valid(g) and g % 3 != 0
 
         turn(0)
         regroup(0)
         turn(1)
         make_gain()
-        for g in range(-1, GROUPS + 3):
+        for g in range(-1, GROUPS):
             if valid(g + 1):
                 quantise(g + 1)
                 decode(g + 1)
             if valid(g):
                 first_stats_vector(g)
-                first_sums_scalar(g)
             if valid(g + 2):
                 regroup(g + 2)
             if valid(g + 3):
                 turn(g + 3)
-            if valid(g):
-                first_mean_scalar(g)
-                first_devs_scalar(g)
             if valid(g - 2):
-                second_mean(g - 2)
                 second_devs(g - 2)
             if valid(g):
                 first_rstd(g)
             if valid(g - 2):
                 second_rstd(g - 2)
+            if scalar_takes(g + 1):
+                first_sums_scalar(g + 1)
+                first_mean_scalar(g + 1)
+                first_devs_scalar(g + 1)
             if valid(g - 1):
                 residual(g - 1)
             if valid(g):
                 first_apply(g)
+            if valid(g - 1):
+                second_mean(g - 1)
             if valid(g - 3):
                 finish(g - 3)
+
+        last = GROUPS - 1
+        half = GROUP // 2
+        second_devs(last - 1)
+        second_rstd(last - 1)
+        finish(last - 2)
+        residual(last, 0, half)
+        second_mean(last, 0, half)
+        residual(last, half, GROUP)
+        second_mean(last, half, GROUP)
+        second_devs(last, 0, half)
+        second_rstd(last, 0, half)
+        second_devs(last, half, GROUP)
+        second_rstd(last, half, GROUP)
+        finish_on_vector(last - 1)
+        finish_on_vector(last, 0, half)
+        finish_on_vector(last, half, GROUP)

@@ -47,7 +47,7 @@ def tile_bdhlayer_pc_t_kernel(
     with tc.tile_pool(name="const", bufs=1) as const, tc.tile_pool(
         name="inputs", bufs=LOADS
     ) as inputs, tc.tile_pool(name="quant", bufs=3) as quant, tc.tile_pool(
-        name="rows", bufs=6
+        name="rows", bufs=GROUPS
     ) as rows, tc.tile_pool(name="small", bufs=6) as small, tc.psum_pool(
         name="turned_banks", bufs=PSUM_BANKS // 2
     ) as turned_banks, tc.psum_pool(

@@ -78,8 +78,10 @@ def tile_bdhlayer_pc_t_kernel(
         w_scales = const.tile([P, D], U8, name="w_scales", align_bytes=64)
         nc.vector.memset(w_scales[:].bitcast(I32), 0)
         w_words = const.tile([P, 2 * D], U8, name="w_words", align_bytes=64)
-        activity = const.tile([P, D], BF16, name="activity")
-        trained = const.tile([P, D], BF16, name="trained")
+        vectors = const.tile([P, 2 * D], BF16, name="vectors")
+        nc.vector.memset(vectors[:], 0.0)
+        ones = const.tile([P, P], BF16, name="ones")
+        nc.vector.memset(ones[:], 1.0)
 
         load(0)
         nc.sync.dma_start(out=w_words[:].bitcast(I32), in_=decoder_words[0].bitcast(I32))
@@ -88,22 +90,31 @@ def tile_bdhlayer_pc_t_kernel(
                 out=w_scales[32 * quadrant : 32 * quadrant + 4, :].bitcast(I32),
                 in_=decoder_scales[0, 4 * quadrant : 4 * quadrant + 4, :].bitcast(I32),
             )
-        nc.sync.dma_start(out=activity[:], in_=running_activity.partition_broadcast(P))
-        nc.sync.dma_start(out=trained[:], in_=scale.partition_broadcast(P))
+        nc.sync.dma_start(out=vectors[0:1, 0:D], in_=running_activity.rearrange("(o d) -> o d", o=1))
+        nc.sync.dma_start(out=vectors[0:1, D : 2 * D], in_=scale.rearrange("(o d) -> o d", o=1))
         for n in range(1, LOADS):
             load(n)
 
         gain = const.tile([P, D], F32, name="gain")
 
-        def make_gain():
+        def spread_vectors():
+            spread = decoded_banks.tile([P, BANK_TILES, D], F32, name="decoded")
+            nc.tensor.matmul(
+                out=spread[:].rearrange("p i d -> p (i d)"), lhsT=ones[:], rhs=vectors[:], start=True, stop=True
+            )
+            return spread
+
+        def make_gain(spread):
             nc.scalar.activation(
                 out=gain[:],
-                in_=activity[:],
+                in_=spread[:, 0, :],
                 func=ACT.Abs_reciprocal_sqrt,
                 scale=1.0 / TARGET_ACTIVITY,
                 bias=1e-6 / TARGET_ACTIVITY,
             )
-            nc.gpsimd.tensor_tensor(out=gain[:], in0=gain[:], in1=trained[:], op=ALU.mult)
+
+        def scale_gain(spread):
+            nc.vector.tensor_tensor(out=gain[:], in0=gain[:], in1=spread[:, 1, :], op=ALU.mult)
 
         def turn(g):
             first_tile = g * GROUP
@@ -335,8 +346,9 @@ def tile_bdhlayer_pc_t_kernel(
 
         turn(0)
         regroup(0)
+        spread = spread_vectors()
         turn(1)
-        make_gain()
+        make_gain(spread)
         for g in range(-1, GROUPS):
             if valid(g + 1):
                 quantise(g + 1)
@@ -359,6 +371,8 @@ def tile_bdhlayer_pc_t_kernel(
                 first_devs_scalar(g + 1)
             if valid(g - 1):
                 residual(g - 1)
+            if g == 0:
+                scale_gain(spread)
             if valid(g):
                 first_apply(g)
             if valid(g - 1):

@@ -25,6 +25,7 @@ GROUP = 4
 GROUPS = TILES // GROUP
 BANK_TILES = 2
 BANKS = GROUP // BANK_TILES
+WARM_PASSES = 5
 PSUM_BANKS = 8
 BN_STATS_DIM = 6
 MEAN = 1
@@ -62,12 +63,15 @@ def tile_bdhlayer_pc_t_kernel(
         row_of = {}
         stat_of = {}
 
-        def load(n):
+        def load_flat(n):
             tiles = slice(n * LOAD_TILES, (n + 1) * LOAD_TILES)
             flat = inputs.tile([P, LOAD_TILES, HEADS, HEAD_DIM], BF16, name="flat")
             for h in range(HEADS):
                 nc.sync.dma_start(out=flat[:, :, h, :], in_=xy_view[h, :, tiles, :])
             flat_of[n] = flat
+
+        def load_x(n):
+            tiles = slice(n * LOAD_TILES, (n + 1) * LOAD_TILES)
             x_sb = inputs.tile([P, LOAD_TILES, D], BF16, name="x_sb")
             nc.sync.dma_start(out=x_sb[:], in_=x_view[:, tiles, :])
             x_of[n] = x_sb
@@ -80,10 +84,17 @@ def tile_bdhlayer_pc_t_kernel(
         w_words = const.tile([P, 2 * D], U8, name="w_words", align_bytes=64)
         vectors = const.tile([P, 2 * D], BF16, name="vectors")
         nc.vector.memset(vectors[:], 0.0)
-        ones = const.tile([P, P], BF16, name="ones")
+        ones = const.tile([P, 2 * D], BF16, name="ones")
         nc.vector.memset(ones[:], 1.0)
+        idle_bank = turned_banks.tile([P, BANK_TILES, 2, P], F32, name="turned")
+        for repeat in range(WARM_PASSES):
+            nc.tensor.matmul(
+                out=idle_bank[:].rearrange("p i u r -> p (i u r)"), lhsT=ones[:, 0:P], rhs=ones[:], start=True, stop=True
+            )
+        warm = const.tile([P, 1], F32, name="warm")
+        nc.scalar.activation(out=warm[:], in_=ones[:, 0:1], func=ACT.Abs_reciprocal_sqrt)
 
-        load(0)
+        load_flat(0)
         nc.sync.dma_start(out=w_words[:].bitcast(I32), in_=decoder_words[0].bitcast(I32))
         for quadrant in range(4):
             nc.sync.dma_start(
@@ -93,14 +104,16 @@ def tile_bdhlayer_pc_t_kernel(
         nc.sync.dma_start(out=vectors[0:1, 0:D], in_=running_activity.rearrange("(o d) -> o d", o=1))
         nc.sync.dma_start(out=vectors[0:1, D : 2 * D], in_=scale.rearrange("(o d) -> o d", o=1))
         for n in range(1, LOADS):
-            load(n)
+            load_flat(n)
+            load_x(n - 1)
+        load_x(LOADS - 1)
 
         gain = const.tile([P, D], F32, name="gain")
 
         def spread_vectors():
             spread = decoded_banks.tile([P, BANK_TILES, D], F32, name="decoded")
             nc.tensor.matmul(
-                out=spread[:].rearrange("p i d -> p (i d)"), lhsT=ones[:], rhs=vectors[:], start=True, stop=True
+                out=spread[:].rearrange("p i d -> p (i d)"), lhsT=ones[:, 0:P], rhs=vectors[:], start=True, stop=True
             )
             return spread
 

@@ -25,6 +25,7 @@ GROUP = 4
 GROUPS = TILES // GROUP
 BANK_TILES = 2
 BANKS = GROUP // BANK_TILES
+GPSIMD_TILES = 3
 WARM_PASSES = 5
 PSUM_BANKS = 8
 BN_STATS_DIM = 6
@@ -321,19 +322,32 @@ def tile_bdhlayer_pc_t_kernel(
         def finish(g):
             row = row_of[g]
             rstd2 = stat_of[g]["rstd2"]
+            neg_mean = stat_of[g]["neg_mean"]
             shift = small.tile([P, GROUP], F32, name="shift")
-            nc.gpsimd.tensor_tensor(
-                out=shift[:], in0=stat_of[g]["neg_mean"][:], in1=rstd2[:], op=ALU.mult
-            )
             for j in range(GROUP):
-                nc.gpsimd.tensor_scalar(
-                    out=row[:, j, :],
-                    in0=row[:, j, :],
-                    scalar1=rstd2[:, j : j + 1],
-                    scalar2=shift[:, j : j + 1],
-                    op0=ALU.mult,
-                    op1=ALU.add,
-                )
+                if j < GPSIMD_TILES:
+                    nc.gpsimd.tensor_scalar(
+                        out=row[:, j, :],
+                        in0=row[:, j, :],
+                        scalar1=neg_mean[:, j : j + 1],
+                        scalar2=rstd2[:, j : j + 1],
+                        op0=ALU.add,
+                        op1=ALU.mult,
+                    )
+                else:
+                    nc.scalar.activation(
+                        out=shift[:, j : j + 1],
+                        in_=neg_mean[:, j : j + 1],
+                        func=ACT.Copy,
+                        scale=rstd2[:, j : j + 1],
+                    )
+                    nc.scalar.activation(
+                        out=row[:, j, :],
+                        in_=row[:, j, :],
+                        func=ACT.Identity,
+                        scale=rstd2[:, j : j + 1],
+                        bias=shift[:, j : j + 1],
+                    )
                 if j % 2 == 1:
                     store(g, j - 1)
 

@@ -25,7 +25,6 @@ GROUP = 4
 GROUPS = TILES // GROUP
 BANK_TILES = 2
 BANKS = GROUP // BANK_TILES
-GPSIMD_TILES = 3
 WARM_PASSES = 5
 PSUM_BANKS = 8
 BN_STATS_DIM = 6
@@ -190,7 +189,7 @@ def tile_bdhlayer_pc_t_kernel(
                         stop=True,
                     )
                 decoded_of[g].append(decoded)
-            stats = small.tile([P, GROUP, BN_STATS_DIM // 2], F32, name="stats")
+            stats = small.tile([P, 2 * GROUP, BN_STATS_DIM // 2], F32, name="stats")
             stat_of[g] = {"stats": stats}
 
         def first_stats_vector(g):
@@ -201,25 +200,16 @@ def tile_bdhlayer_pc_t_kernel(
                     in_=decoded_of[g][b][:].rearrange("p i d -> p d i"),
                 )
 
-        def first_sums_scalar(g):
-            y_sum = small.tile([P, BANK_TILES], F32, name="y_sum")
+        def first_mean_scalar(g):
             for i in range(BANK_TILES):
                 unused = quant.tile([P, D], BF16, name="unused")
                 nc.scalar.activation(
                     out=unused[:],
                     in_=decoded_of[g][1][:, i, :],
                     func=ACT.Identity,
-                    accum_out=y_sum[:, i : i + 1],
+                    scale=1.0 / D,
+                    accum_out=stat_of[g]["stats"][:, BANK_TILES + i, MEAN : MEAN + 1],
                 )
-            stat_of[g]["y_sum"] = y_sum
-
-        def first_mean_scalar(g):
-            nc.scalar.activation(
-                out=stat_of[g]["stats"][:, BANK_TILES:GROUP, MEAN],
-                in_=stat_of[g]["y_sum"][:],
-                func=ACT.Copy,
-                scale=1.0 / D,
-            )
 
         def first_devs_scalar(g):
             for i in range(BANK_TILES):
@@ -233,16 +223,19 @@ def tile_bdhlayer_pc_t_kernel(
                     accum_out=stat_of[g]["stats"][:, BANK_TILES + i, DEVIATIONS : DEVIATIONS + 1],
                 )
 
-        def first_rstd(g):
-            rstd1 = small.tile([P, GROUP], F32, name="rstd1")
+        def first_rstd(g, with_second):
+            width = 2 * GROUP if with_second else GROUP
+            rstd = small.tile([P, 2 * GROUP], F32, name="rstd")
             nc.scalar.activation(
-                out=rstd1[:],
-                in_=stat_of[g]["stats"][:, :, DEVIATIONS],
+                out=rstd[:, 0:width],
+                in_=stat_of[g]["stats"][:, 0:width, DEVIATIONS],
                 func=ACT.Abs_reciprocal_sqrt,
                 scale=1.0 / D,
                 bias=EPS_LN,
             )
-            stat_of[g]["rstd1"] = rstd1
+            stat_of[g]["rstd1"] = rstd[:, 0:GROUP]
+            if with_second:
+                stat_of[g - 2]["rstd2"] = rstd[:, GROUP : 2 * GROUP]
 
         def first_apply(g):
             row = rows.tile([P, GROUP, D], F32, name="row")
@@ -287,12 +280,15 @@ def tile_bdhlayer_pc_t_kernel(
                 scalar1=-1.0 / D,
             )
 
-        def second_devs(g, first=0, last=GROUP):
+        def second_devs(g, first=0, last=GROUP, beside_first=False):
             if first == 0:
                 squares = quant.tile([P, GROUP, D], BF16, name="squares")
-                dev2 = small.tile([P, GROUP], F32, name="dev2")
                 stat_of[g]["squares"] = squares
-                stat_of[g]["dev2"] = dev2
+                if beside_first:
+                    stat_of[g]["dev2"] = stat_of[g + 2]["stats"][:, GROUP : 2 * GROUP, DEVIATIONS]
+                else:
+                    dev2 = small.tile([P, GROUP], F32, name="dev2")
+                    stat_of[g]["dev2"] = dev2
             for j in range(first, last):
                 nc.scalar.activation(
                     out=stat_of[g]["squares"][:, j, :],
@@ -319,13 +315,14 @@ def tile_bdhlayer_pc_t_kernel(
                 out=out_view[:, g * GROUP + j : g * GROUP + j + 2, :], in_=row_of[g][:, j : j + 2, :]
             )
 
-        def finish(g):
+        def finish(g, scalar_helps):
             row = row_of[g]
             rstd2 = stat_of[g]["rstd2"]
             neg_mean = stat_of[g]["neg_mean"]
             shift = small.tile([P, GROUP], F32, name="shift")
+            gpsimd_tiles = GROUP - 1 if scalar_helps else GROUP
             for j in range(GROUP):
-                if j < GPSIMD_TILES:
+                if j < gpsimd_tiles:
                     nc.gpsimd.tensor_scalar(
                         out=row[:, j, :],
                         in0=row[:, j, :],
@@ -369,7 +366,7 @@ def tile_bdhlayer_pc_t_kernel(
             return 0 <= g < GROUPS
 
         def scalar_takes(g):
-            return valid(g) and g % 3 != 0
+            return valid(g) and g % 4 != 0
 
         turn(0)
         regroup(0)
@@ -387,13 +384,10 @@ def tile_bdhlayer_pc_t_kernel(
             if valid(g + 3):
                 turn(g + 3)
             if valid(g - 2):
-                second_devs(g - 2)
+                second_devs(g - 2, beside_first=True)
             if valid(g):
-                first_rstd(g)
-            if valid(g - 2):
-                second_rstd(g - 2)
+                first_rstd(g, valid(g - 2))
             if scalar_takes(g + 1):
-                first_sums_scalar(g + 1)
                 first_mean_scalar(g + 1)
                 first_devs_scalar(g + 1)
             if valid(g - 1):
@@ -405,13 +399,13 @@ def tile_bdhlayer_pc_t_kernel(
             if valid(g - 1):
                 second_mean(g - 1)
             if valid(g - 3):
-                finish(g - 3)
+                finish(g - 3, not scalar_takes(g + 1))
 
         last = GROUPS - 1
         half = GROUP // 2
         second_devs(last - 1)
         second_rstd(last - 1)
-        finish(last - 2)
+        finish(last - 2, False)
         residual(last, 0, half)
         second_mean(last, 0, half)
         residual(last, half, GROUP)

@@ -25,6 +25,7 @@ GROUP = 4
 GROUPS = TILES // GROUP
 BANK_TILES = 2
 BANKS = GROUP // BANK_TILES
+ALL_BANKS = (0, 1)
 WARM_PASSES = 5
 PSUM_BANKS = 8
 BN_STATS_DIM = 6
@@ -63,11 +64,16 @@ def tile_bdhlayer_pc_t_kernel(
         row_of = {}
         stat_of = {}
 
-        def load_flat(n):
-            tiles = slice(n * LOAD_TILES, (n + 1) * LOAD_TILES)
+        def load_flat(n, pieces=1):
             flat = inputs.tile([P, LOAD_TILES, HEADS, HEAD_DIM], BF16, name="flat")
-            for h in range(HEADS):
-                nc.sync.dma_start(out=flat[:, :, h, :], in_=xy_view[h, :, tiles, :])
+            width = LOAD_TILES // pieces
+            for piece in range(pieces):
+                first = n * LOAD_TILES + piece * width
+                for h in range(HEADS):
+                    nc.sync.dma_start(
+                        out=flat[:, piece * width : (piece + 1) * width, h, :],
+                        in_=xy_view[h, :, first : first + width, :],
+                    )
             flat_of[n] = flat
 
         def load_x(n):
@@ -94,7 +100,7 @@ def tile_bdhlayer_pc_t_kernel(
         warm = const.tile([P, 1], F32, name="warm")
         nc.scalar.activation(out=warm[:], in_=ones[:, 0:1], func=ACT.Abs_reciprocal_sqrt)
 
-        load_flat(0)
+        load_flat(0, pieces=BANKS)
         nc.sync.dma_start(out=w_words[:].bitcast(I32), in_=decoder_words[0].bitcast(I32))
         for quadrant in range(4):
             nc.sync.dma_start(
@@ -129,12 +135,11 @@ def tile_bdhlayer_pc_t_kernel(
         def scale_gain(spread):
             nc.vector.tensor_tensor(out=gain[:], in0=gain[:], in1=spread[:, 1, :], op=ALU.mult)
 
-        def turn(g):
+        def turn(g, banks=ALL_BANKS):
             first_tile = g * GROUP
             words = flat_of[first_tile // LOAD_TILES][:].rearrange("p j h n -> p (j h n)").bitcast(F32)
             row_words = K // 2
-            turned_of[g] = []
-            for b in range(BANKS):
+            for b in banks:
                 turned = turned_banks.tile([P, BANK_TILES, 2, P], F32, name="turned")
                 for i in range(BANK_TILES):
                     first = (first_tile % LOAD_TILES + b * BANK_TILES + i) * row_words
@@ -144,37 +149,42 @@ def tile_bdhlayer_pc_t_kernel(
                             words[:, first + u : first + row_words : 2],
                             ident[:],
                         )
-                turned_of[g].append(turned)
+                turned_of[g, b] = turned
 
-        def regroup(g):
-            grouped = quant.tile([P, GROUP, P, PACK], BF16, name="grouped", align_bytes=64)
+        def regroup(g, banks=ALL_BANKS):
+            if banks[0] == 0:
+                grouped = quant.tile([P, GROUP, P, PACK], BF16, name="grouped", align_bytes=64)
+                grouped_of[g] = grouped
             grouped_words = (
-                grouped[:]
+                grouped_of[g][:]
                 .rearrange("p j r t -> p (j r t)")
                 .bitcast(F32)
                 .rearrange("p (j r u) -> p j r u", j=GROUP, u=2)
             )
-            for b in range(BANKS):
+            for b in banks:
                 nc.scalar.copy(
                     out=grouped_words[:, b * BANK_TILES : (b + 1) * BANK_TILES, :, :],
-                    in_=turned_of[g][b][:].rearrange("p i u r -> p i r u"),
+                    in_=turned_of[g, b][:].rearrange("p i u r -> p i r u"),
                 )
-            grouped_of[g] = grouped
 
-        def quantise(g):
-            codes = quant.tile([P, GROUP * P], U32, name="codes", align_bytes=64)
-            code_scales = quant.tile([P, GROUP * P], U8, name="code_scales", align_bytes=64)
-            nc.vector.quantize_mx(
-                out=codes[:].bitcast(FP8X4),
-                scales=code_scales[:],
-                in_=grouped_of[g][:].rearrange("p j r t -> p (j r t)"),
-            )
-            codes_of[g] = (codes, code_scales)
-
-        def decode(g):
+        def quantise(g, banks=ALL_BANKS):
+            if banks[0] == 0:
+                codes = quant.tile([P, GROUP * P], U32, name="codes", align_bytes=64)
+                code_scales = quant.tile([P, GROUP * P], U8, name="code_scales", align_bytes=64)
+                codes_of[g] = (codes, code_scales)
             codes, code_scales = codes_of[g]
-            decoded_of[g] = []
-            for b in range(BANKS):
+            tokens = slice(banks[0] * BANK_TILES * P, (banks[-1] + 1) * BANK_TILES * P)
+            nc.vector.quantize_mx(
+                out=codes[:, tokens].bitcast(FP8X4),
+                scales=code_scales[:, tokens],
+                in_=grouped_of[g][:].rearrange("p j r t -> p (j r t)")[:, tokens.start * PACK : tokens.stop * PACK],
+            )
+
+        def decode(g, banks=ALL_BANKS):
+            codes, code_scales = codes_of[g]
+            if banks[0] == 0:
+                decoded_of[g] = []
+            for b in banks:
                 decoded = decoded_banks.tile([P, BANK_TILES, D], F32, name="decoded")
                 for i in range(BANK_TILES):
                     j = b * BANK_TILES + i
@@ -189,8 +199,9 @@ def tile_bdhlayer_pc_t_kernel(
                         stop=True,
                     )
                 decoded_of[g].append(decoded)
-            stats = small.tile([P, 2 * GROUP, BN_STATS_DIM // 2], F32, name="stats")
-            stat_of[g] = {"stats": stats}
+            if banks[0] == 0:
+                stats = small.tile([P, 2 * GROUP, BN_STATS_DIM // 2], F32, name="stats")
+                stat_of[g] = {"stats": stats}
 
         def first_stats_vector(g):
             stats = stat_of[g]["stats"]
@@ -368,12 +379,28 @@ def tile_bdhlayer_pc_t_kernel(
         def scalar_takes(g):
             return valid(g) and g % 4 != 0
 
-        turn(0)
-        regroup(0)
+        for b in ALL_BANKS:
+            turn(0, (b,))
+            regroup(0, (b,))
         spread = spread_vectors()
-        turn(1)
+        for b in ALL_BANKS:
+            quantise(0, (b,))
+            decode(0, (b,))
+            turn(1, (b,))
         make_gain(spread)
-        for g in range(-1, GROUPS):
+        regroup(1)
+        turn(2)
+        first_stats_vector(0)
+        regroup(2)
+        turn(3)
+        first_rstd(0, False)
+        scale_gain(spread)
+        first_apply(0)
+        quantise(1)
+        decode(1)
+        first_mean_scalar(1)
+        first_devs_scalar(1)
+        for g in range(1, GROUPS):
             if valid(g + 1):
                 quantise(g + 1)
                 decode(g + 1)
@@ -392,8 +419,6 @@ def tile_bdhlayer_pc_t_kernel(
                 first_devs_scalar(g + 1)
             if valid(g - 1):
                 residual(g - 1)
-            if g == 0:
-                scale_gain(spread)
             if valid(g):
                 first_apply(g)
             if valid(g - 1):

@@ -250,7 +250,7 @@ def tile_bdhlayer_pc_t_kernel(
 
         def first_apply(g):
             row = rows.tile([P, GROUP, D], F32, name="row")
-            for b in range(BANKS):
+            for b in reversed(ALL_BANKS) if scalar_takes(g) else ALL_BANKS:
                 for i in range(BANK_TILES):
                     j = b * BANK_TILES + i
                     nc.vector.scalar_tensor_tensor(
@@ -321,6 +321,13 @@ def tile_bdhlayer_pc_t_kernel(
                 bias=EPS_LN,
             )
 
+        def second_shift(g):
+            shift = small.tile([P, GROUP], F32, name="shift")
+            nc.vector.tensor_tensor(
+                out=shift[:], in0=stat_of[g]["neg_mean"][:], in1=stat_of[g]["rstd2"], op=ALU.mult
+            )
+            stat_of[g]["shift"] = shift
+
         def store(g, j):
             nc.sync.dma_start(
                 out=out_view[:, g * GROUP + j : g * GROUP + j + 2, :], in_=row_of[g][:, j : j + 2, :]
@@ -329,26 +336,19 @@ def tile_bdhlayer_pc_t_kernel(
         def finish(g, scalar_helps):
             row = row_of[g]
             rstd2 = stat_of[g]["rstd2"]
-            neg_mean = stat_of[g]["neg_mean"]
-            shift = small.tile([P, GROUP], F32, name="shift")
+            shift = stat_of[g]["shift"]
             gpsimd_tiles = GROUP - 1 if scalar_helps else GROUP
             for j in range(GROUP):
                 if j < gpsimd_tiles:
                     nc.gpsimd.tensor_scalar(
                         out=row[:, j, :],
                         in0=row[:, j, :],
-                        scalar1=neg_mean[:, j : j + 1],
-                        scalar2=rstd2[:, j : j + 1],
-                        op0=ALU.add,
-                        op1=ALU.mult,
+                        scalar1=rstd2[:, j : j + 1],
+                        scalar2=shift[:, j : j + 1],
+                        op0=ALU.mult,
+                        op1=ALU.add,
                     )
                 else:
-                    nc.scalar.activation(
-                        out=shift[:, j : j + 1],
-                        in_=neg_mean[:, j : j + 1],
-                        func=ACT.Copy,
-                        scale=rstd2[:, j : j + 1],
-                    )
                     nc.scalar.activation(
                         out=row[:, j, :],
                         in_=row[:, j, :],
@@ -404,21 +404,24 @@ def tile_bdhlayer_pc_t_kernel(
             if valid(g + 1):
                 quantise(g + 1)
                 decode(g + 1)
-            if valid(g):
-                first_stats_vector(g)
             if valid(g + 2):
                 regroup(g + 2)
             if valid(g + 3):
                 turn(g + 3)
             if valid(g - 2):
                 second_devs(g - 2, beside_first=True)
+            if valid(g - 1):
+                residual(g - 1, 0, GROUP - 1)
+            if valid(g - 3):
+                second_shift(g - 3)
+            if valid(g - 1):
+                residual(g - 1, GROUP - 1, GROUP)
             if valid(g):
+                first_stats_vector(g)
                 first_rstd(g, valid(g - 2))
             if scalar_takes(g + 1):
                 first_mean_scalar(g + 1)
                 first_devs_scalar(g + 1)
-            if valid(g - 1):
-                residual(g - 1)
             if valid(g):
                 first_apply(g)
             if valid(g - 1):
@@ -430,6 +433,7 @@ def tile_bdhlayer_pc_t_kernel(
         half = GROUP // 2
         second_devs(last - 1)
         second_rstd(last - 1)
+        second_shift(last - 2)
         finish(last - 2, False)
         residual(last, 0, half)
         second_mean(last, 0, half)

@@ -401,13 +401,13 @@ def tile_bdhlayer_pc_t_kernel(
         first_mean_scalar(1)
         first_devs_scalar(1)
         for g in range(1, GROUPS):
+            if valid(g + 3):
+                turn(g + 3)
             if valid(g + 1):
                 quantise(g + 1)
                 decode(g + 1)
             if valid(g + 2):
                 regroup(g + 2)
-            if valid(g + 3):
-                turn(g + 3)
             if valid(g - 2):
                 second_devs(g - 2, beside_first=True)
             if valid(g - 1):

@@ -101,17 +101,19 @@ def tile_bdhlayer_pc_t_kernel(
         nc.scalar.activation(out=warm[:], in_=ones[:, 0:1], func=ACT.Abs_reciprocal_sqrt)
 
         load_flat(0, pieces=BANKS)
+        load_flat(1)
         nc.sync.dma_start(out=w_words[:].bitcast(I32), in_=decoder_words[0].bitcast(I32))
         for quadrant in range(4):
             nc.sync.dma_start(
                 out=w_scales[32 * quadrant : 32 * quadrant + 4, :].bitcast(I32),
                 in_=decoder_scales[0, 4 * quadrant : 4 * quadrant + 4, :].bitcast(I32),
             )
-        nc.sync.dma_start(out=vectors[0:1, 0:D], in_=running_activity.rearrange("(o d) -> o d", o=1))
-        nc.sync.dma_start(out=vectors[0:1, D : 2 * D], in_=scale.rearrange("(o d) -> o d", o=1))
-        for n in range(1, LOADS):
+        nc.gpsimd.dma_start(out=vectors[0:1, 0:D], in_=running_activity.rearrange("(o d) -> o d", o=1))
+        nc.gpsimd.dma_start(out=vectors[0:1, D : 2 * D], in_=scale.rearrange("(o d) -> o d", o=1))
+        for n in range(2, LOADS):
             load_flat(n)
-            load_x(n - 1)
+            load_x(n - 2)
+        load_x(LOADS - 2)
         load_x(LOADS - 1)
 
         gain = const.tile([P, D], F32, name="gain")
@@ -382,22 +384,22 @@ def tile_bdhlayer_pc_t_kernel(
         for b in ALL_BANKS:
             turn(0, (b,))
             regroup(0, (b,))
-        spread = spread_vectors()
         for b in ALL_BANKS:
             quantise(0, (b,))
             decode(0, (b,))
-            turn(1, (b,))
+        spread = spread_vectors()
+        turn(1)
         make_gain(spread)
         regroup(1)
         turn(2)
         first_stats_vector(0)
         regroup(2)
-        turn(3)
         first_rstd(0, False)
         scale_gain(spread)
         first_apply(0)
         quantise(1)
         decode(1)
+        turn(3)
         first_mean_scalar(1)
         first_devs_scalar(1)
         for g in range(1, GROUPS):

@@ -26,7 +26,7 @@ GROUPS = TILES // GROUP
 BANK_TILES = 2
 BANKS = GROUP // BANK_TILES
 ALL_BANKS = (0, 1)
-WARM_PASSES = 5
+WARM_PASSES = 2
 PSUM_BANKS = 8
 BN_STATS_DIM = 6
 MEAN = 1
@@ -207,33 +207,36 @@ def tile_bdhlayer_pc_t_kernel(
 
         def first_stats_vector(g):
             stats = stat_of[g]["stats"]
-            for b in range(BANKS - 1 if scalar_takes(g) else BANKS):
+            for b in range(BANKS - scalar_banks(g)):
                 nc.vector.bn_stats(
                     out=stats[:, b * BANK_TILES : (b + 1) * BANK_TILES, :].rearrange("p i s -> p (i s)"),
                     in_=decoded_of[g][b][:].rearrange("p i d -> p d i"),
                 )
 
+        def scalar_tiles(g):
+            return range((BANKS - scalar_banks(g)) * BANK_TILES, GROUP)
+
         def first_mean_scalar(g):
-            for i in range(BANK_TILES):
+            for j in scalar_tiles(g):
                 unused = quant.tile([P, D], BF16, name="unused")
                 nc.scalar.activation(
                     out=unused[:],
-                    in_=decoded_of[g][1][:, i, :],
+                    in_=decoded_of[g][j // BANK_TILES][:, j % BANK_TILES, :],
                     func=ACT.Identity,
                     scale=1.0 / D,
-                    accum_out=stat_of[g]["stats"][:, BANK_TILES + i, MEAN : MEAN + 1],
+                    accum_out=stat_of[g]["stats"][:, j, MEAN : MEAN + 1],
                 )
 
         def first_devs_scalar(g):
-            for i in range(BANK_TILES):
+            for j in scalar_tiles(g):
                 unused = quant.tile([P, D], BF16, name="unused")
                 nc.scalar.activation(
                     out=unused[:],
-                    in_=decoded_of[g][1][:, i, :],
+                    in_=decoded_of[g][j // BANK_TILES][:, j % BANK_TILES, :],
                     func=ACT.Square,
                     scale=-1.0,
-                    bias=stat_of[g]["stats"][:, BANK_TILES + i, MEAN : MEAN + 1],
-                    accum_out=stat_of[g]["stats"][:, BANK_TILES + i, DEVIATIONS : DEVIATIONS + 1],
+                    bias=stat_of[g]["stats"][:, j, MEAN : MEAN + 1],
+                    accum_out=stat_of[g]["stats"][:, j, DEVIATIONS : DEVIATIONS + 1],
                 )
 
         def first_rstd(g, with_second):
@@ -252,7 +255,7 @@ def tile_bdhlayer_pc_t_kernel(
 
         def first_apply(g):
             row = rows.tile([P, GROUP, D], F32, name="row")
-            for b in reversed(ALL_BANKS) if scalar_takes(g) else ALL_BANKS:
+            for b in reversed(ALL_BANKS) if scalar_banks(g) > 0 else ALL_BANKS:
                 for i in range(BANK_TILES):
                     j = b * BANK_TILES + i
                     nc.vector.scalar_tensor_tensor(
@@ -282,6 +285,29 @@ def tile_bdhlayer_pc_t_kernel(
                     op1=ALU.add,
                     accum_out=stat_of[g]["row_sum"][:, j : j + 1],
                 )
+
+        def residual_alone(g):
+            row = row_of[g]
+            first_tile = g * GROUP
+            x_sb = x_of[first_tile // LOAD_TILES]
+            for j in range(GROUP):
+                nc.vector.scalar_tensor_tensor(
+                    out=row[:, j, :],
+                    in0=row[:, j, :],
+                    scalar=stat_of[g]["rstd1"][:, j : j + 1],
+                    in1=x_sb[:, first_tile % LOAD_TILES + j, :],
+                    op0=ALU.mult,
+                    op1=ALU.add,
+                )
+            last_stats = small.tile([P, GROUP, BN_STATS_DIM // 2], F32, name="last_stats")
+            stat_of[g]["last_stats"] = last_stats
+
+        def second_stats_vector(g, b):
+            tiles = slice(b * BANK_TILES, (b + 1) * BANK_TILES)
+            nc.vector.bn_stats(
+                out=stat_of[g]["last_stats"][:, tiles, :].rearrange("p i s -> p (i s)"),
+                in_=row_of[g][:, tiles, :].rearrange("p i d -> p d i"),
+            )
 
         def second_mean(g, first=0, last=GROUP):
             if first == 0:
@@ -326,7 +352,7 @@ def tile_bdhlayer_pc_t_kernel(
         def second_shift(g):
             shift = small.tile([P, GROUP], F32, name="shift")
             nc.vector.tensor_tensor(
-                out=shift[:], in0=stat_of[g]["neg_mean"][:], in1=stat_of[g]["rstd2"], op=ALU.mult
+                out=shift[:], in0=stat_of[g]["neg_mean"][:], in1=stat_of[g]["rstd2"][:, 0:GROUP], op=ALU.mult
             )
             stat_of[g]["shift"] = shift
 
@@ -335,12 +361,11 @@ def tile_bdhlayer_pc_t_kernel(
                 out=out_view[:, g * GROUP + j : g * GROUP + j + 2, :], in_=row_of[g][:, j : j + 2, :]
             )
 
-        def finish(g, scalar_helps):
+        def finish(g, gpsimd_tiles, tiles=range(GROUP)):
             row = row_of[g]
             rstd2 = stat_of[g]["rstd2"]
             shift = stat_of[g]["shift"]
-            gpsimd_tiles = GROUP - 1 if scalar_helps else GROUP
-            for j in range(GROUP):
+            for j in tiles:
                 if j < gpsimd_tiles:
                     nc.gpsimd.tensor_scalar(
                         out=row[:, j, :],
@@ -361,15 +386,19 @@ def tile_bdhlayer_pc_t_kernel(
                 if j % 2 == 1:
                     store(g, j - 1)
 
-        def finish_on_vector(g, first=0, last=GROUP):
+        def finish_on_vector(g, tiles):
             row = row_of[g]
-            for j in range(first, last):
+            for j in tiles:
+                if g == GROUPS - 1:
+                    mean, take = stat_of[g]["last_stats"][:, j, MEAN : MEAN + 1], ALU.subtract
+                else:
+                    mean, take = stat_of[g]["neg_mean"][:, j : j + 1], ALU.add
                 nc.vector.tensor_scalar(
                     out=row[:, j, :],
                     in0=row[:, j, :],
-                    scalar1=stat_of[g]["neg_mean"][:, j : j + 1],
+                    scalar1=mean,
                     scalar2=stat_of[g]["rstd2"][:, j : j + 1],
-                    op0=ALU.add,
+                    op0=take,
                     op1=ALU.mult,
                 )
                 if j % 2 == 1:
@@ -378,8 +407,8 @@ def tile_bdhlayer_pc_t_kernel(
         def valid(g):
             return 0 <= g < GROUPS
 
-        def scalar_takes(g):
-            return valid(g) and g % 4 != 0
+        def scalar_banks(g):
+            return min(g % 4, 1)
 
         for b in ALL_BANKS:
             turn(0, (b,))
@@ -411,7 +440,9 @@ def tile_bdhlayer_pc_t_kernel(
             if valid(g + 2):
                 regroup(g + 2)
             if valid(g - 2):
-                second_devs(g - 2, beside_first=True)
+                second_devs(g - 2, beside_first=g < GROUPS - 1)
+            if g == GROUPS - 1:
+                second_rstd(g - 2)
             if valid(g - 1):
                 residual(g - 1, 0, GROUP - 1)
             if valid(g - 3):
@@ -420,8 +451,8 @@ def tile_bdhlayer_pc_t_kernel(
                 residual(g - 1, GROUP - 1, GROUP)
             if valid(g):
                 first_stats_vector(g)
-                first_rstd(g, valid(g - 2))
-            if scalar_takes(g + 1):
+                first_rstd(g, valid(g - 2) and g < GROUPS - 1)
+            if valid(g + 1):
                 first_mean_scalar(g + 1)
                 first_devs_scalar(g + 1)
             if valid(g):
@@ -429,22 +460,23 @@ def tile_bdhlayer_pc_t_kernel(
             if valid(g - 1):
                 second_mean(g - 1)
             if valid(g - 3):
-                finish(g - 3, not scalar_takes(g + 1))
+                finish(g - 3, GROUP if scalar_banks(g + 1) > 0 else GROUP - 1)
 
         last = GROUPS - 1
         half = GROUP // 2
+        second_shift(last - 2)
+        finish(last - 2, 0, range(half))
         second_devs(last - 1)
         second_rstd(last - 1)
-        second_shift(last - 2)
-        finish(last - 2, False)
-        residual(last, 0, half)
-        second_mean(last, 0, half)
-        residual(last, half, GROUP)
-        second_mean(last, half, GROUP)
-        second_devs(last, 0, half)
+        residual_alone(last)
+        finish_on_vector(last - 2, range(half, GROUP))
+        for b in ALL_BANKS:
+            second_stats_vector(last, b)
+        stat_of[last]["dev2"] = stat_of[last]["last_stats"][:, :, DEVIATIONS]
         second_rstd(last, 0, half)
-        second_devs(last, half, GROUP)
         second_rstd(last, half, GROUP)
-        finish_on_vector(last - 1)
-        finish_on_vector(last, 0, half)
-        finish_on_vector(last, half, GROUP)
+        second_shift(last - 1)
+        finish_on_vector(last, range(half))
+        finish_on_vector(last - 1, range(half))
+        finish(last - 1, 0, range(half, GROUP))
+        finish_on_vector(last, range(half, GROUP))

@@ -408,7 +408,7 @@ def tile_bdhlayer_pc_t_kernel(
             return 0 <= g < GROUPS
 
         def scalar_banks(g):
-            return min(g % 4, 1)
+            return 1 if 0 < g < GROUPS else 0
 
         for b in ALL_BANKS:
             turn(0, (b,))

import concourse.mybir as mybir
from concourse.masks import make_identity

F32 = mybir.dt.float32
BF16 = mybir.dt.bfloat16
I32 = mybir.dt.int32
U32 = mybir.dt.uint32
U8 = mybir.dt.uint8
FP8X4 = mybir.dt.float8_e4m3fn_x4
FP4X4 = mybir.dt.float4_e2m1fn_x4
ALU = mybir.AluOpType
ACT = mybir.ActivationFunctionType

P = 128
HEADS = 2
HEAD_DIM = 256
K = HEADS * HEAD_DIM
PACK = 4
D = 256
T = 8192
TILES = T // P
LOAD_TILES = 4
LOADS = TILES // LOAD_TILES
GROUP = 4
GROUPS = TILES // GROUP
BANK_TILES = 2
BANKS = GROUP // BANK_TILES
ALL_BANKS = (0, 1)
WARM_PASSES = 2
PSUM_BANKS = 8
BN_STATS_DIM = 6
MEAN = 1
DEVIATIONS = 2
EPS_LN = 1e-5
TARGET_ACTIVITY = 0.1

FLOPS = 2 * T * K * D


def tile_bdhlayer_pc_t_kernel(
    tc, xy_sparse, decoder_words, decoder_scales, x, scale, running_activity, out
):
    nc = tc.nc

    xy_view = xy_sparse[0].rearrange("h (p j) n -> h p j n", p=P)
    x_view = x[0, 0].rearrange("(p j) d -> p j d", p=P)
    out_view = out[0, 0].rearrange("(p j) d -> p j d", p=P)

    with tc.tile_pool(name="const", bufs=1) as const, tc.tile_pool(
        name="inputs", bufs=LOADS
    ) as inputs, tc.tile_pool(name="quant", bufs=3) as quant, tc.tile_pool(
        name="rows", bufs=GROUPS
    ) as rows, tc.tile_pool(name="small", bufs=6) as small, tc.psum_pool(
        name="turned_banks", bufs=PSUM_BANKS // 2
    ) as turned_banks, tc.psum_pool(
        name="decoded_banks", bufs=PSUM_BANKS // 2
    ) as decoded_banks, tc.manual_schedule():
        flat_of = {}
        x_of = {}
        turned_of = {}
        grouped_of = {}
        codes_of = {}
        decoded_of = {}
        row_of = {}
        stat_of = {}

        def load_flat(n, pieces=1):
            flat = inputs.tile([P, LOAD_TILES, HEADS, HEAD_DIM], BF16, name="flat")
            width = LOAD_TILES // pieces
            for piece in range(pieces):
                first = n * LOAD_TILES + piece * width
                for h in range(HEADS):
                    nc.sync.dma_start(
                        out=flat[:, piece * width : (piece + 1) * width, h, :],
                        in_=xy_view[h, :, first : first + width, :],
                    )
            flat_of[n] = flat

        def load_x(n):
            tiles = slice(n * LOAD_TILES, (n + 1) * LOAD_TILES)
            x_sb = inputs.tile([P, LOAD_TILES, D], BF16, name="x_sb")
            nc.sync.dma_start(out=x_sb[:], in_=x_view[:, tiles, :])
            x_of[n] = x_sb

        ident = const.tile([P, P], F32, name="ident")
        make_identity(nc, ident[:])

        w_scales = const.tile([P, D], U8, name="w_scales", align_bytes=64)
        nc.vector.memset(w_scales[:].bitcast(I32), 0)
        w_words = const.tile([P, 2 * D], U8, name="w_words", align_bytes=64)
        vectors = const.tile([P, 2 * D], BF16, name="vectors")
        nc.vector.memset(vectors[:], 0.0)
        ones = const.tile([P, 2 * D], BF16, name="ones")
        nc.vector.memset(ones[:], 1.0)
        idle_bank = turned_banks.tile([P, BANK_TILES, 2, P], F32, name="turned")
        for repeat in range(WARM_PASSES):
            nc.tensor.matmul(
                out=idle_bank[:].rearrange("p i u r -> p (i u r)"), lhsT=ones[:, 0:P], rhs=ones[:], start=True, stop=True
            )
        warm = const.tile([P, 1], F32, name="warm")
        nc.scalar.activation(out=warm[:], in_=ones[:, 0:1], func=ACT.Abs_reciprocal_sqrt)

        load_flat(0, pieces=BANKS)
        load_flat(1)
        nc.sync.dma_start(out=w_words[:].bitcast(I32), in_=decoder_words[0].bitcast(I32))
        for quadrant in range(4):
            nc.sync.dma_start(
                out=w_scales[32 * quadrant : 32 * quadrant + 4, :].bitcast(I32),
                in_=decoder_scales[0, 4 * quadrant : 4 * quadrant + 4, :].bitcast(I32),
            )
        nc.gpsimd.dma_start(out=vectors[0:1, 0:D], in_=running_activity.rearrange("(o d) -> o d", o=1))
        nc.gpsimd.dma_start(out=vectors[0:1, D : 2 * D], in_=scale.rearrange("(o d) -> o d", o=1))
        for n in range(2, LOADS):
            load_flat(n)
            load_x(n - 2)
        load_x(LOADS - 2)
        load_x(LOADS - 1)

        gain = const.tile([P, D], F32, name="gain")

        def spread_vectors():
            spread = decoded_banks.tile([P, BANK_TILES, D], F32, name="decoded")
            nc.tensor.matmul(
                out=spread[:].rearrange("p i d -> p (i d)"), lhsT=ones[:, 0:P], rhs=vectors[:], start=True, stop=True
            )
            return spread

        def make_gain(spread):
            nc.scalar.activation(
                out=gain[:],
                in_=spread[:, 0, :],
                func=ACT.Abs_reciprocal_sqrt,
                scale=1.0 / TARGET_ACTIVITY,
                bias=1e-6 / TARGET_ACTIVITY,
            )

        def scale_gain(spread):
            nc.vector.tensor_tensor(out=gain[:], in0=gain[:], in1=spread[:, 1, :], op=ALU.mult)

        def turn(g, banks=ALL_BANKS):
            first_tile = g * GROUP
            words = flat_of[first_tile // LOAD_TILES][:].rearrange("p j h n -> p (j h n)").bitcast(F32)
            row_words = K // 2
            for b in banks:
                turned = turned_banks.tile([P, BANK_TILES, 2, P], F32, name="turned")
                for i in range(BANK_TILES):
                    first = (first_tile % LOAD_TILES + b * BANK_TILES + i) * row_words
                    for u in range(2):
                        nc.tensor.transpose(
                            turned[:, i, u, :],
                            words[:, first + u : first + row_words : 2],
                            ident[:],
                        )
                turned_of[g, b] = turned

        def regroup(g, banks=ALL_BANKS):
            if banks[0] == 0:
                grouped = quant.tile([P, GROUP, P, PACK], BF16, name="grouped", align_bytes=64)
                grouped_of[g] = grouped
            grouped_words = (
                grouped_of[g][:]
                .rearrange("p j r t -> p (j r t)")
                .bitcast(F32)
                .rearrange("p (j r u) -> p j r u", j=GROUP, u=2)
            )
            for b in banks:
                nc.scalar.copy(
                    out=grouped_words[:, b * BANK_TILES : (b + 1) * BANK_TILES, :, :],
                    in_=turned_of[g, b][:].rearrange("p i u r -> p i r u"),
                )

        def quantise(g, banks=ALL_BANKS):
            if banks[0] == 0:
                codes = quant.tile([P, GROUP * P], U32, name="codes", align_bytes=64)
                code_scales = quant.tile([P, GROUP * P], U8, name="code_scales", align_bytes=64)
                codes_of[g] = (codes, code_scales)
            codes, code_scales = codes_of[g]
            tokens = slice(banks[0] * BANK_TILES * P, (banks[-1] + 1) * BANK_TILES * P)
            nc.vector.quantize_mx(
                out=codes[:, tokens].bitcast(FP8X4),
                scales=code_scales[:, tokens],
                in_=grouped_of[g][:].rearrange("p j r t -> p (j r t)")[:, tokens.start * PACK : tokens.stop * PACK],
            )

        def decode(g, banks=ALL_BANKS):
            codes, code_scales = codes_of[g]
            if banks[0] == 0:
                decoded_of[g] = []
            for b in banks:
                decoded = decoded_banks.tile([P, BANK_TILES, D], F32, name="decoded")
                for i in range(BANK_TILES):
                    j = b * BANK_TILES + i
                    tokens = slice(j * P, (j + 1) * P)
                    nc.tensor.matmul_mx(
                        out=decoded[:, i, :],
                        lhsT=codes[:, tokens].bitcast(FP8X4),
                        lhsT_scale=code_scales[:, tokens],
                        rhs=w_words[:].bitcast(FP4X4),
                        rhs_scale=w_scales[:],
                        start=True,
                        stop=True,
                    )
                decoded_of[g].append(decoded)
            if banks[0] == 0:
                stats = small.tile([P, 2 * GROUP, BN_STATS_DIM // 2], F32, name="stats")
                stat_of[g] = {"stats": stats}

        def first_stats_vector(g):
            stats = stat_of[g]["stats"]
            for b in range(BANKS - scalar_banks(g)):
                nc.vector.bn_stats(
                    out=stats[:, b * BANK_TILES : (b + 1) * BANK_TILES, :].rearrange("p i s -> p (i s)"),
                    in_=decoded_of[g][b][:].rearrange("p i d -> p d i"),
                )

        def scalar_tiles(g):
            return range((BANKS - scalar_banks(g)) * BANK_TILES, GROUP)

        def first_mean_scalar(g):
            for j in scalar_tiles(g):
                unused = quant.tile([P, D], BF16, name="unused")
                nc.scalar.activation(
                    out=unused[:],
                    in_=decoded_of[g][j // BANK_TILES][:, j % BANK_TILES, :],
                    func=ACT.Identity,
                    scale=1.0 / D,
                    accum_out=stat_of[g]["stats"][:, j, MEAN : MEAN + 1],
                )

        def first_devs_scalar(g):
            for j in scalar_tiles(g):
                unused = quant.tile([P, D], BF16, name="unused")
                nc.scalar.activation(
                    out=unused[:],
                    in_=decoded_of[g][j // BANK_TILES][:, j % BANK_TILES, :],
                    func=ACT.Square,
                    scale=-1.0,
                    bias=stat_of[g]["stats"][:, j, MEAN : MEAN + 1],
                    accum_out=stat_of[g]["stats"][:, j, DEVIATIONS : DEVIATIONS + 1],
                )

        def first_rstd(g, with_second):
            width = 2 * GROUP if with_second else GROUP
            rstd = small.tile([P, 2 * GROUP], F32, name="rstd")
            nc.scalar.activation(
                out=rstd[:, 0:width],
                in_=stat_of[g]["stats"][:, 0:width, DEVIATIONS],
                func=ACT.Abs_reciprocal_sqrt,
                scale=1.0 / D,
                bias=EPS_LN,
            )
            stat_of[g]["rstd1"] = rstd[:, 0:GROUP]
            if with_second:
                stat_of[g - 2]["rstd2"] = rstd[:, GROUP : 2 * GROUP]

        def first_apply(g):
            row = rows.tile([P, GROUP, D], F32, name="row")
            for b in reversed(ALL_BANKS) if scalar_banks(g) > 0 else ALL_BANKS:
                for i in range(BANK_TILES):
                    j = b * BANK_TILES + i
                    nc.vector.scalar_tensor_tensor(
                        out=row[:, j, :],
                        in0=decoded_of[g][b][:, i, :],
                        scalar=stat_of[g]["stats"][:, j, MEAN : MEAN + 1],
                        in1=gain[:],
                        op0=ALU.subtract,
                        op1=ALU.mult,
                    )
            row_of[g] = row

        def residual(g, first=0, last=GROUP):
            row = row_of[g]
            first_tile = g * GROUP
            x_sb = x_of[first_tile // LOAD_TILES]
            if first == 0:
                row_sum = small.tile([P, GROUP], F32, name="row_sum")
                stat_of[g]["row_sum"] = row_sum
            for j in range(first, last):
                nc.vector.scalar_tensor_tensor(
                    out=row[:, j, :],
                    in0=row[:, j, :],
                    scalar=stat_of[g]["rstd1"][:, j : j + 1],
                    in1=x_sb[:, first_tile % LOAD_TILES + j, :],
                    op0=ALU.mult,
                    op1=ALU.add,
                    accum_out=stat_of[g]["row_sum"][:, j : j + 1],
                )

        def residual_alone(g):
            row = row_of[g]
            first_tile = g * GROUP
            x_sb = x_of[first_tile // LOAD_TILES]
            for j in range(GROUP):
                nc.vector.scalar_tensor_tensor(
                    out=row[:, j, :],
                    in0=row[:, j, :],
                    scalar=stat_of[g]["rstd1"][:, j : j + 1],
                    in1=x_sb[:, first_tile % LOAD_TILES + j, :],
                    op0=ALU.mult,
                    op1=ALU.add,
                )
            last_stats = small.tile([P, GROUP, BN_STATS_DIM // 2], F32, name="last_stats")
            stat_of[g]["last_stats"] = last_stats

        def second_stats_vector(g, b):
            tiles = slice(b * BANK_TILES, (b + 1) * BANK_TILES)
            nc.vector.bn_stats(
                out=stat_of[g]["last_stats"][:, tiles, :].rearrange("p i s -> p (i s)"),
                in_=row_of[g][:, tiles, :].rearrange("p i d -> p d i"),
            )

        def second_mean(g, first=0, last=GROUP):
            if first == 0:
                neg_mean = small.tile([P, GROUP], F32, name="neg_mean")
                stat_of[g]["neg_mean"] = neg_mean
            nc.vector.tensor_scalar_mul(
                out=stat_of[g]["neg_mean"][:, first:last],
                in0=stat_of[g]["row_sum"][:, first:last],
                scalar1=-1.0 / D,
            )

        def second_devs(g, first=0, last=GROUP, beside_first=False):
            if first == 0:
                squares = quant.tile([P, GROUP, D], BF16, name="squares")
                stat_of[g]["squares"] = squares
                if beside_first:
                    stat_of[g]["dev2"] = stat_of[g + 2]["stats"][:, GROUP : 2 * GROUP, DEVIATIONS]
                else:
                    dev2 = small.tile([P, GROUP], F32, name="dev2")
                    stat_of[g]["dev2"] = dev2
            for j in range(first, last):
                nc.scalar.activation(
                    out=stat_of[g]["squares"][:, j, :],
                    in_=row_of[g][:, j, :],
                    func=ACT.Square,
                    bias=stat_of[g]["neg_mean"][:, j : j + 1],
                    accum_out=stat_of[g]["dev2"][:, j : j + 1],
                )

        def second_rstd(g, first=0, last=GROUP):
            if first == 0:
                rstd2 = small.tile([P, GROUP], F32, name="rstd2")
                stat_of[g]["rstd2"] = rstd2
            nc.scalar.activation(
                out=stat_of[g]["rstd2"][:, first:last],
                in_=stat_of[g]["dev2"][:, first:last],
                func=ACT.Abs_reciprocal_sqrt,
                scale=1.0 / D,
                bias=EPS_LN,
            )

        def second_shift(g):
            shift = small.tile([P, GROUP], F32, name="shift")
            nc.vector.tensor_tensor(
                out=shift[:], in0=stat_of[g]["neg_mean"][:], in1=stat_of[g]["rstd2"][:, 0:GROUP], op=ALU.mult
            )
            stat_of[g]["shift"] = shift

        def store(g, j):
            nc.sync.dma_start(
                out=out_view[:, g * GROUP + j : g * GROUP + j + 2, :], in_=row_of[g][:, j : j + 2, :]
            )

        def finish(g, gpsimd_tiles, tiles=range(GROUP)):
            row = row_of[g]
            rstd2 = stat_of[g]["rstd2"]
            shift = stat_of[g]["shift"]
            for j in tiles:
                if j < gpsimd_tiles:
                    nc.gpsimd.tensor_scalar(
                        out=row[:, j, :],
                        in0=row[:, j, :],
                        scalar1=rstd2[:, j : j + 1],
                        scalar2=shift[:, j : j + 1],
                        op0=ALU.mult,
                        op1=ALU.add,
                    )
                else:
                    nc.scalar.activation(
                        out=row[:, j, :],
                        in_=row[:, j, :],
                        func=ACT.Identity,
                        scale=rstd2[:, j : j + 1],
                        bias=shift[:, j : j + 1],
                    )
                if j % 2 == 1:
                    store(g, j - 1)

        def finish_on_vector(g, tiles):
            row = row_of[g]
            for j in tiles:
                if g == GROUPS - 1:
                    mean, take = stat_of[g]["last_stats"][:, j, MEAN : MEAN + 1], ALU.subtract
                else:
                    mean, take = stat_of[g]["neg_mean"][:, j : j + 1], ALU.add
                nc.vector.tensor_scalar(
                    out=row[:, j, :],
                    in0=row[:, j, :],
                    scalar1=mean,
                    scalar2=stat_of[g]["rstd2"][:, j : j + 1],
                    op0=take,
                    op1=ALU.mult,
                )
                if j % 2 == 1:
                    store(g, j - 1)

        def valid(g):
            return 0 <= g < GROUPS

        def scalar_banks(g):
            return 1 if 0 < g < GROUPS else 0

        for b in ALL_BANKS:
            turn(0, (b,))
            regroup(0, (b,))
        for b in ALL_BANKS:
            quantise(0, (b,))
            decode(0, (b,))
        spread = spread_vectors()
        turn(1)
        make_gain(spread)
        regroup(1)
        turn(2)
        first_stats_vector(0)
        regroup(2)
        first_rstd(0, False)
        scale_gain(spread)
        first_apply(0)
        quantise(1)
        decode(1)
        turn(3)
        first_mean_scalar(1)
        first_devs_scalar(1)
        for g in range(1, GROUPS):
            if valid(g + 3):
                turn(g + 3)
            if valid(g + 1):
                quantise(g + 1)
                decode(g + 1)
            if valid(g + 2):
                regroup(g + 2)
            if valid(g - 2):
                second_devs(g - 2, beside_first=g < GROUPS - 1)
            if g == GROUPS - 1:
                second_rstd(g - 2)
            if valid(g - 1):
                residual(g - 1, 0, GROUP - 1)
            if valid(g - 3):
                second_shift(g - 3)
            if valid(g - 1):
                residual(g - 1, GROUP - 1, GROUP)
            if valid(g):
                first_stats_vector(g)
                first_rstd(g, valid(g - 2) and g < GROUPS - 1)
            if valid(g + 1):
                first_mean_scalar(g + 1)
                first_devs_scalar(g + 1)
            if valid(g):
                first_apply(g)
            if valid(g - 1):
                second_mean(g - 1)
            if valid(g - 3):
                finish(g - 3, GROUP if scalar_banks(g + 1) > 0 else GROUP - 1)

        last = GROUPS - 1
        half = GROUP // 2
        second_shift(last - 2)
        finish(last - 2, 0, range(half))
        second_devs(last - 1)
        second_rstd(last - 1)
        residual_alone(last)
        finish_on_vector(last - 2, range(half, GROUP))
        for b in ALL_BANKS:
            second_stats_vector(last, b)
        stat_of[last]["dev2"] = stat_of[last]["last_stats"][:, :, DEVIATIONS]
        second_rstd(last, 0, half)
        second_rstd(last, half, GROUP)
        second_shift(last - 1)
        finish_on_vector(last, range(half))
        finish_on_vector(last - 1, range(half))
        finish(last - 1, 0, range(half, GROUP))
        finish_on_vector(last, range(half, GROUP))
